import numpy as np
import ml_dtypes


def mxq(x, axis, fmt="e4m3"):
    dtype, down = {"e4m3": (ml_dtypes.float8_e4m3fn, 7), "e5m2": (ml_dtypes.float8_e5m2, 14)}[fmt]
    v = np.moveaxis(np.asarray(x, np.float32).astype(ml_dtypes.bfloat16).astype(np.float64), axis, -1)
    blocks = v.reshape(v.shape[:-1] + (-1, 32))
    amax = np.abs(blocks).max(-1, keepdims=True)
    byte = np.maximum(np.where(amax > 0, np.frexp(amax)[1] - 1 + 127, 0) - down, 1)
    scale = np.exp2(byte - 127.0)
    codes = (blocks / scale).astype(np.float32).astype(dtype).astype(np.float64)
    return np.moveaxis((codes * scale).reshape(v.shape), -1, axis)


WIDE = False


def mx_kscale(k):
    if not WIDE:
        return np.ones(k)
    levels = np.array([10, -10, 5, -5, 0])
    a = np.random.permutation(np.resize(levels, k // 512 * 4)).reshape(k // 512, 4)
    idx = np.arange(k)
    return np.exp2(a[idx // 512, idx % 128 // 32])


BF16 = ml_dtypes.bfloat16


def bf(x):
    return np.asarray(x, np.float32).astype(BF16)


def f64(x):
    return np.asarray(x).astype(np.float64)


B, IN, G, OUT = 512, 2048, 8, 512
K = IN * G
GRID_MIN, GRID_MAX = -2.0, 2.0
H = (GRID_MAX - GRID_MIN) / (G - 1)


def setup_inputs():
    sf = mx_kscale(K)[::G]
    a = np.log2(sf.max() / sf)
    grid = bf(np.linspace(GRID_MIN, GRID_MAX, G) + 0.02 * np.random.standard_normal(G))
    z = np.random.standard_normal((B, IN))
    far = f64(grid).max() + H * np.sqrt(a * np.log(2.0)) + 0.05 * z
    x = np.where(a > 0, far, z)
    w = np.random.standard_normal((K, OUT)) / np.sqrt(IN) * np.repeat(np.exp2(a), G)[:, None]
    return {"x": bf(x), "grid": grid, "spline_weight": bf(w)}


def reference(x, grid, spline_weight):
    h = (GRID_MAX - GRID_MIN) / (G - 1)
    basis = np.exp(-np.square((f64(x)[..., None] - f64(grid)) / h))
    return mxq(basis.reshape(basis.shape[0], -1), 1, "e4m3") @ mxq(f64(spline_weight), 0, "e4m3")

@@ -1,0 +1,162 @@
+from contextlib import ExitStack
+
+import concourse.mybir as mybir
+from concourse.masks import make_identity
+
+F32 = mybir.dt.float32
+BF16 = mybir.dt.bfloat16
+U32 = mybir.dt.uint32
+U8 = mybir.dt.uint8
+FP8X4 = mybir.dt.float8_e4m3fn_x4
+ACT = mybir.ActivationFunctionType
+ALU = mybir.AluOpType
+
+P = 128
+B, IN, G, OUT = 512, 2048, 8, 512
+K = IN * G
+FLOPS = 2 * B * K * OUT
+INV_H2 = 49.0 / 16.0
+
+S_HALVES, Q_CHUNKS, A_QUADS, T_PACK, L_HALVES, R_POINTS = 2, 64, 4, 4, 2, 4
+B_TILES = B // P
+
+
+def tile_gaussiankernel_k_kernel(tc, x, grid, spline_weight, out):
+    nc = tc.nc
+    with ExitStack() as ctx:
+        const = ctx.enter_context(tc.tile_pool(name="const", bufs=1))
+        xin = ctx.enter_context(tc.tile_pool(name="xin", bufs=B_TILES))
+        xgrp = ctx.enter_context(tc.tile_pool(name="xgrp", bufs=3))
+        wload = ctx.enter_context(tc.tile_pool(name="wload", bufs=3))
+        work = ctx.enter_context(tc.tile_pool(name="work", bufs=3))
+        store = ctx.enter_context(tc.tile_pool(name="store", bufs=B_TILES))
+        acc_pool = ctx.enter_context(tc.psum_pool(name="acc", bufs=1))
+        xt_pool = ctx.enter_context(tc.psum_pool(name="xt", bufs=4))
+
+        g_bf = const.tile([P, R_POINTS], BF16)
+        for l in range(L_HALVES):
+            nc.sync.dma_start(
+                out=g_bf[l:P:L_HALVES, :],
+                in_=grid[R_POINTS * l : R_POINTS * (l + 1)].partition_broadcast(Q_CHUNKS),
+            )
+        g = const.tile([P, R_POINTS], F32)
+        nc.vector.tensor_copy(out=g[:], in_=g_bf[:])
+        neg_g = const.tile([P, R_POINTS], F32)
+        nc.vector.tensor_scalar_mul(out=neg_g[:], in0=g[:], scalar1=-1.0)
+        two_g = const.tile([P, R_POINTS], F32)
+        nc.vector.tensor_scalar_mul(out=two_g[:], in0=g[:], scalar1=2.0)
+        neg_g2_h2 = const.tile([P, R_POINTS], F32)
+        nc.vector.scalar_tensor_tensor(
+            out=neg_g2_h2[:], in0=g[:], scalar=-INV_H2, in1=g[:], op0=ALU.mult, op1=ALU.mult
+        )
+
+        ident = const.tile([P, P], F32)
+        make_identity(nc, ident[:])
+
+        x_twice = []
+        for bt in range(B_TILES):
+            x_rows = xin.tile([P, IN], BF16)
+            nc.sync.dma_start(out=x_rows[:], in_=x[bt * P : (bt + 1) * P, :])
+            twice = xin.tile([P, 8, P, L_HALVES], F32, name="twice")
+            nc.vector.tensor_copy(
+                out=twice[:],
+                in_=x_rows[:]
+                .bitcast(F32)
+                .rearrange("b (Q c) -> b c Q", c=8)
+                .unsqueeze(3)
+                .to_broadcast([P, 8, P, L_HALVES]),
+            )
+            x_twice.append(twice)
+
+        acc = [acc_pool.tile([P, OUT], F32, name="acc%d" % bt) for bt in range(B_TILES)]
+
+        w_view = spline_weight.rearrange(
+            "(s q a t l r) o -> s a l q t (r o)",
+            s=S_HALVES, q=Q_CHUNKS, a=A_QUADS, t=T_PACK, l=L_HALVES, r=R_POINTS,
+        )
+
+        n_pass = S_HALVES * A_QUADS * R_POINTS
+        i_pass = 0
+        for s in range(S_HALVES):
+            for a in range(A_QUADS):
+                w_raw = wload.tile([P, T_PACK, R_POINTS, OUT], BF16)
+                for l in range(L_HALVES):
+                    nc.sync.dma_start(
+                        out=w_raw[l:P:L_HALVES].rearrange("q t r o -> q t (r o)"),
+                        in_=w_view[s, a, l],
+                    )
+
+                xq = xgrp.tile([P, B * T_PACK], BF16)
+                xq_words = xq[:].bitcast(F32).rearrange("p (b u) -> p b u", u=2)
+                for h in range(2):
+                    xt = xt_pool.tile([P, 2, 2 * P], F32)
+                    for u in range(2):
+                        for e in range(2):
+                            nc.tensor.transpose(
+                                xt[:, u, e * P : (e + 1) * P],
+                                x_twice[2 * h + e][
+                                    :, 2 * a + u, Q_CHUNKS * s : Q_CHUNKS * (s + 1), :
+                                ].rearrange("b q l -> b (q l)"),
+                                ident[:],
+                            )
+                    nc.scalar.copy(
+                        out=xq_words[:, 2 * P * h : 2 * P * (h + 1), :],
+                        in_=xt[:].rearrange("p u b -> p b u"),
+                    )
+
+                for r in range(R_POINTS):
+                    w_grouped = work.tile([P, OUT, T_PACK], BF16, align_bytes=64)
+                    nc.vector.tensor_copy(
+                        out=w_grouped[:].rearrange("p (c i) t -> p c t i", i=4),
+                        in_=w_raw[:, :, r, :].rearrange("p t (c i) -> p c t i", i=4),
+                    )
+                    w_codes = work.tile([P, OUT], U32, align_bytes=64)
+                    w_scales = work.tile([P, OUT], U8, align_bytes=64)
+                    nc.vector.quantize_mx(
+                        out=w_codes[:].bitcast(FP8X4),
+                        scales=w_scales[:],
+                        in_=w_grouped[:].rearrange("p o t -> p (o t)"),
+                    )
+
+                    quad = work.tile([P, B * T_PACK], F32)
+                    basis = work.tile([P, B * T_PACK], BF16, align_bytes=64)
+                    if r % 2 == 0:
+                        nc.scalar.activation(
+                            out=quad[:], in_=xq[:], func=ACT.Square, bias=neg_g[:, r : r + 1], scale=1.0
+                        )
+                        nc.scalar.activation(out=basis[:], in_=quad[:], func=ACT.Exp, scale=-INV_H2)
+                    else:
+                        nc.vector.scalar_tensor_tensor(
+                            out=quad[:], in0=xq[:], scalar=two_g[:, r : r + 1], in1=xq[:],
+                            op0=ALU.subtract, op1=ALU.mult,
+                        )
+                        nc.scalar.activation(
+                            out=basis[:], in_=quad[:], func=ACT.Exp,
+                            bias=neg_g2_h2[:, r : r + 1], scale=-INV_H2,
+                        )
+                    b_codes = work.tile([P, B], U32, align_bytes=64)
+                    b_scales = work.tile([P, B], U8, align_bytes=64)
+                    nc.vector.quantize_mx(
+                        out=b_codes[:].bitcast(FP8X4), scales=b_scales[:], in_=basis[:]
+                    )
+
+                    for bt in range(B_TILES):
+                        b_cols = slice(bt * P, (bt + 1) * P)
+                        nc.tensor.matmul_mx(
+                            out=acc[bt][:],
+                            lhsT=b_codes[:, b_cols].bitcast(FP8X4),
+                            lhsT_scale=b_scales[:, b_cols],
+                            rhs=w_codes[:].bitcast(FP8X4),
+                            rhs_scale=w_scales[:],
+                            start=(i_pass == 0),
+                            stop=(i_pass == n_pass - 1),
+                        )
+                    i_pass += 1
+
+        for bt in range(B_TILES):
+            result = store.tile([P, OUT], F32)
+            if bt % 2 == 0:
+                nc.vector.tensor_copy(out=result[:], in_=acc[bt][:])
+            else:
+                nc.scalar.copy(out=result[:], in_=acc[bt][:])
+            nc.sync.dma_start(out=out[bt * P : (bt + 1) * P, :], in_=result[:])

@@ -10,6 +10,7 @@ U8 = mybir.dt.uint8
 FP8X4 = mybir.dt.float8_e4m3fn_x4
 ACT = mybir.ActivationFunctionType
 ALU = mybir.AluOpType
+AX = mybir.AxisListType
 
 P = 128
 B, IN, G, OUT = 512, 2048, 8, 512
@@ -19,26 +20,85 @@ INV_H2 = 49.0 / 16.0
 
 S_HALVES, Q_CHUNKS, A_QUADS, T_PACK, L_HALVES, R_POINTS = 2, 64, 4, 4, 2, 4
 B_TILES = B // P
+COLS = B * T_PACK
+
+ON_SCALAR, ON_VECTOR, MIXED = 0, 1, 2
 
 
 def tile_gaussiankernel_k_kernel(tc, x, grid, spline_weight, out):
     nc = tc.nc
+    groups = [(a, s) for a in range(A_QUADS) for s in range(S_HALVES)]
+    passes = []
+    for g in range(len(groups)):
+        if g % 2 == 0:
+            plan = [(3, ON_SCALAR), (1, MIXED), (0, ON_VECTOR), (2, MIXED)]
+        elif g < len(groups) - 1:
+            plan = [
+                (2, ON_SCALAR),
+                (0, ON_VECTOR),
+                (1, MIXED),
+                (3, ON_VECTOR if g % 4 == 1 else ON_SCALAR),
+            ]
+        else:
+            plan = [(2, ON_SCALAR), (0, ON_VECTOR), (3, ON_SCALAR), (1, MIXED)]
+        passes += [(g, r, how) for r, how in plan]
+    n_pass = len(passes)
+
     with ExitStack() as ctx:
         const = ctx.enter_context(tc.tile_pool(name="const", bufs=1))
         xin = ctx.enter_context(tc.tile_pool(name="xin", bufs=B_TILES))
-        xgrp = ctx.enter_context(tc.tile_pool(name="xgrp", bufs=3))
+        xgrp = ctx.enter_context(tc.tile_pool(name="xgrp", bufs=1))
         wload = ctx.enter_context(tc.tile_pool(name="wload", bufs=3))
-        work = ctx.enter_context(tc.tile_pool(name="work", bufs=3))
+        work = ctx.enter_context(tc.tile_pool(name="work", bufs=4))
         store = ctx.enter_context(tc.tile_pool(name="store", bufs=B_TILES))
         acc_pool = ctx.enter_context(tc.psum_pool(name="acc", bufs=1))
-        xt_pool = ctx.enter_context(tc.psum_pool(name="xt", bufs=4))
+        bank_pool = ctx.enter_context(tc.psum_pool(name="banks", bufs=4))
+        ctx.enter_context(tc.manual_schedule())
+
+        w_view = spline_weight.rearrange(
+            "(s q a t l r) o -> s a l q t r o",
+            s=S_HALVES, q=Q_CHUNKS, a=A_QUADS, t=T_PACK, l=L_HALVES, r=R_POINTS,
+        )
+        w_raw = {}
+
+        def load_w(g):
+            a, s = groups[g]
+            w_raw[g] = wload.tile([P, T_PACK, R_POINTS, OUT], BF16, name="w_raw")
+            for l in range(L_HALVES):
+                nc.sync.dma_start(
+                    out=w_raw[g][l:P:L_HALVES].rearrange("q t r o -> q t (r o)"),
+                    in_=w_view[s, a, l].rearrange("q t r o -> q t (r o)"),
+                )
+
+        def load_w_pass(i):
+            g_, r, how = passes[i]
+            a, s = groups[g_]
+            if g_ not in w_raw:
+                w_raw[g_] = wload.tile([P, T_PACK, R_POINTS, OUT], BF16, name="w_raw")
+            for l in range(L_HALVES):
+                nc.sync.dma_start(out=w_raw[g_][l:P:L_HALVES, :, r, :], in_=w_view[s, a, l, :, :, r, :])
 
         g_bf = const.tile([P, R_POINTS], BF16)
         for l in range(L_HALVES):
-            nc.sync.dma_start(
+            nc.scalar.dma_start(
                 out=g_bf[l:P:L_HALVES, :],
                 in_=grid[R_POINTS * l : R_POINTS * (l + 1)].partition_broadcast(Q_CHUNKS),
             )
+        g_all_bf = const.tile([P, G], BF16)
+        nc.scalar.dma_start(out=g_all_bf[:], in_=grid.partition_broadcast(P))
+        x_rows = [xin.tile([P, S_HALVES, IN // S_HALVES], BF16, name="x_rows") for bt in range(B_TILES)]
+        for s in range(S_HALVES):
+            for bt in range(B_TILES):
+                nc.sync.dma_start(
+                    out=x_rows[bt][:, s, :],
+                    in_=x[bt * P : (bt + 1) * P, s * (IN // S_HALVES) : (s + 1) * (IN // S_HALVES)],
+                )
+            for i in range(2 * s, 2 * s + 2):
+                load_w_pass(i)
+        load_w(1)
+
+        ident = const.tile([P, P], F32)
+        make_identity(nc, ident[:])
         g = const.tile([P, R_POINTS], F32)
         nc.vector.tensor_copy(out=g[:], in_=g_bf[:])
         neg_g = const.tile([P, R_POINTS], F32)
@@ -50,113 +110,259 @@ def tile_gaussiankernel_k_kernel(tc, x, grid, spline_weight, out):
             out=neg_g2_h2[:], in0=g[:], scalar=-INV_H2, in1=g[:], op0=ALU.mult, op1=ALU.mult
         )
 
-        ident = const.tile([P, P], F32)
-        make_identity(nc, ident[:])
+        def words(bt, s):
+            return x_rows[bt][:, s, :].bitcast(F32).rearrange("b (q c) -> b c q", c=8)
 
-        x_twice = []
-        for bt in range(B_TILES):
-            x_rows = xin.tile([P, IN], BF16)
-            nc.sync.dma_start(out=x_rows[:], in_=x[bt * P : (bt + 1) * P, :])
-            twice = xin.tile([P, 8, P, L_HALVES], F32, name="twice")
-            nc.vector.tensor_copy(
-                out=twice[:],
-                in_=x_rows[:]
-                .bitcast(F32)
-                .rearrange("b (Q c) -> b c Q", c=8)
-                .unsqueeze(3)
-                .to_broadcast([P, 8, P, L_HALVES]),
+        def turn_half(words_of, h):
+            bank = bank_pool.tile([P, 2, 2 * P], F32, name="bank")
+            for u in range(2):
+                for e in range(2):
+                    nc.tensor.transpose(bank[:, u, e * P : (e + 1) * P], words_of(2 * h + e, u), ident[:])
+            return bank
+
+        def copy_half(dst, bank, h):
+            nc.scalar.copy(
+                out=dst[:].bitcast(F32).rearrange("p (b u) -> p b u", u=2)[:, 2 * P * h : 2 * P * (h + 1), :],
+                in_=bank[:].rearrange("p u b -> p b u"),
             )
-            x_twice.append(twice)
+
+        xq = [xgrp.tile([P, COLS], BF16, name="xq%d" % i) for i in range(len(groups))]
+
+        def turn_quad(a):
+            def words_of(bt, u):
+                return (
+                    x_rows[bt][:].rearrange("b s i -> b (s i)").bitcast(F32)
+                    .rearrange("b (Q c) -> b c Q", c=8)[:, 2 * a + u, :]
+                )
+
+            return [turn_half(words_of, h) for h in range(2)]
+
+        def spread_quad(a, banks):
+            x_turned = work.tile([P, COLS], BF16, name="x_turned", bufs=2)
+            for h in range(2):
+                copy_half(x_turned, banks[h], h)
+            for g_ in range(len(groups)):
+                if groups[g_][0] == a and g_ > 0:
+                    s = groups[g_][1]
+                    for l in range(L_HALVES):
+                        nc.sync.dma_start(
+                            out=xq[g_][l:P:L_HALVES, :],
+                            in_=x_turned[Q_CHUNKS * s : Q_CHUNKS * (s + 1), :],
+                        )
+
+        w_grouped, w_codes, w_scales, exponent, exponent_0, mixed, basis, b_codes, b_scales = (
+            {}, {}, {}, {}, {}, {}, {}, {}, {}
+        )
+
+        def group_w(i):
+            g_, r, how = passes[i]
+            w_grouped[i] = work.tile([P, OUT, T_PACK], BF16, name="w_grouped", bufs=3, align_bytes=64)
+            nc.vector.tensor_copy(
+                out=w_grouped[i][:].rearrange("p (c i) t -> p c t i", i=4),
+                in_=w_raw[g_][:, :, r, :].rearrange("p t (c i) -> p c t i", i=4),
+            )
+
+        def quantise_w(i):
+            w_codes[i] = work.tile([P, OUT], U32, name="w_codes", bufs=7, align_bytes=64)
+            w_scales[i] = work.tile([P, OUT], U8, name="w_scales", bufs=7, align_bytes=64)
+            nc.vector.quantize_mx(
+                out=w_codes[i][:].bitcast(FP8X4),
+                scales=w_scales[i][:],
+                in_=w_grouped[i][:].rearrange("p o t -> p (o t)"),
+            )
+
+        def exponent_on_vector(i):
+            g_, r, how = passes[i]
+            name = "exponent_0" if r == 0 else "exponent"
+            exponent[i] = work.tile([P, COLS], F32, name=name, bufs=2 if r == 0 else 3)
+            if r == 0:
+                exponent_0[g_] = exponent[i]
+            nc.vector.scalar_tensor_tensor(
+                out=exponent[i][:], in0=xq[g_][:], scalar=two_g[:, r : r + 1], in1=xq[g_][:],
+                op0=ALU.subtract, op1=ALU.mult,
+            )
+
+        def exponent_on_scalar(i):
+            g_, r, how = passes[i]
+            exponent[i] = work.tile([P, COLS], F32, name="exponent", bufs=3)
+            nc.scalar.activation(
+                out=exponent[i][:], in_=xq[g_][:], func=ACT.Square, bias=neg_g[:, r : r + 1], scale=1.0
+            )
+
+        def exponent_mixed(i):
+            g_, r, how = passes[i]
+            mixed[i] = []
+            for bt in range(B_TILES):
+                bank = bank_pool.tile([P, P * T_PACK], F32, name="bank")
+                nc.tensor.matmul(
+                    bank[:], lhsT=mix[r][:], rhs=exponent_0[g_][:, bt * P * T_PACK : (bt + 1) * P * T_PACK],
+                    start=True, stop=True,
+                )
+                mixed[i].append(bank)
+
+        def make_basis(i):
+            g_, r, how = passes[i]
+            basis[i] = work.tile([P, COLS], BF16, name="basis", align_bytes=64)
+            if how == ON_SCALAR:
+                nc.scalar.activation(out=basis[i][:], in_=exponent[i][:], func=ACT.Exp, scale=-INV_H2)
+            elif how == ON_VECTOR:
+                nc.scalar.activation(
+                    out=basis[i][:], in_=exponent[i][:], func=ACT.Exp,
+                    bias=neg_g2_h2[:, r : r + 1], scale=-INV_H2,
+                )
+            else:
+                for bt in range(B_TILES):
+                    nc.scalar.activation(
+                        out=basis[i][:, bt * P * T_PACK : (bt + 1) * P * T_PACK], in_=mixed[i][bt][:],
+                        func=ACT.Exp, bias=neg_g2_h2[:, r : r + 1], scale=-INV_H2,
+                    )
+
+        def quantise_b(i):
+            b_codes[i] = work.tile([P, B], U32, name="b_codes", bufs=5, align_bytes=64)
+            b_scales[i] = work.tile([P, B], U8, name="b_scales", bufs=5, align_bytes=64)
+            nc.vector.quantize_mx(
+                out=b_codes[i][:].bitcast(FP8X4), scales=b_scales[i][:], in_=basis[i][:]
+            )
 
         acc = [acc_pool.tile([P, OUT], F32, name="acc%d" % bt) for bt in range(B_TILES)]
 
-        w_view = spline_weight.rearrange(
-            "(s q a t l r) o -> s a l q t (r o)",
-            s=S_HALVES, q=Q_CHUNKS, a=A_QUADS, t=T_PACK, l=L_HALVES, r=R_POINTS,
+        def multiply(i):
+            for bt in range(B_TILES):
+                b_cols = slice(bt * P, (bt + 1) * P)
+                nc.tensor.matmul_mx(
+                    out=acc[bt][:],
+                    lhsT=b_codes[i][:, b_cols].bitcast(FP8X4),
+                    lhsT_scale=b_scales[i][:, b_cols],
+                    rhs=w_codes[i][:].bitcast(FP8X4),
+                    rhs_scale=w_scales[i][:],
+                    start=(i == 0),
+                    stop=False,
+                )
+
+        for h in range(2):
+            x_twice = []
+            for bt in (2 * h, 2 * h + 1):
+                twice = xin.tile([P, 2, Q_CHUNKS, L_HALVES], F32, name="twice")
+                nc.vector.tensor_copy(
+                    out=twice[:],
+                    in_=words(bt, 0)[:, 0:2, :].unsqueeze(3).to_broadcast([P, 2, Q_CHUNKS, L_HALVES]),
+                )
+                x_twice.append(twice)
+            copy_half(
+                xq[0],
+                turn_half(lambda bt, u: x_twice[bt - 2 * h][:, u].rearrange("b q l -> b (q l)"), h),
+                h,
+            )
+            cols = slice(h * COLS // 2, (h + 1) * COLS // 2)
+            if h == 0:
+                exponent[0] = work.tile([P, COLS], F32, name="exponent", bufs=3)
+            nc.scalar.activation(
+                out=exponent[0][:, cols], in_=xq[0][:, cols], func=ACT.Square,
+                bias=neg_g[:, passes[0][1] : passes[0][1] + 1], scale=1.0,
+            )
+
+        g_all = const.tile([P, G], F32)
+        nc.vector.tensor_copy(out=g_all[:], in_=g_all_bf[:])
+        share = const.tile([P, G], F32)
+        nc.vector.tensor_scalar(
+            out=share[:], in0=g_all[:], scalar1=g_all[:, 0:1], scalar2=None, op0=ALU.subtract
         )
+        inv_span = const.tile([P, 1], F32)
+        nc.vector.reciprocal(out=inv_span[:], in_=share[:, R_POINTS : R_POINTS + 1])
+        nc.vector.tensor_scalar_mul(out=share[:], in0=share[:], scalar1=inv_span[:])
+        ident_ql = ident[:].rearrange("p (q l) -> p q l", l=L_HALVES)
+        odd = const.tile([P, 1], F32)
+        nc.vector.reduce_sum(out=odd[:], in_=ident_ql[:, :, 1], axis=AX.X)
+        sign = const.tile([P, 1], F32)
+        nc.vector.tensor_scalar(out=sign[:], in0=odd[:], scalar1=2.0, scalar2=-1.0, op0=ALU.mult, op1=ALU.add)
+        even = const.tile([P, 1], F32)
+        nc.vector.tensor_scalar(out=even[:], in0=odd[:], scalar1=-1.0, scalar2=1.0, op0=ALU.mult, op1=ALU.add)
+        weight = const.tile([P, G], F32)
+        nc.vector.tensor_scalar(
+            out=weight[:], in0=share[:], scalar1=sign[:], scalar2=even[:], op0=ALU.mult, op1=ALU.add
+        )
+        same_q = const.tile([P, Q_CHUNKS], F32)
+        nc.vector.tensor_add(out=same_q[:], in0=ident_ql[:, :, 0], in1=ident_ql[:, :, 1])
+        mix = {}
+        for r in (1, 2):
+            mix[r] = const.tile([P, P], F32, name="mix%d" % r)
+            for l in range(L_HALVES):
+                j = R_POINTS * l + r
+                nc.vector.tensor_scalar_mul(
+                    out=mix[r][:].rearrange("p (q l) -> p q l", l=L_HALVES)[:, :, l],
+                    in0=same_q[:], scalar1=weight[:, j : j + 1],
+                )
 
-        n_pass = S_HALVES * A_QUADS * R_POINTS
-        i_pass = 0
-        for s in range(S_HALVES):
-            for a in range(A_QUADS):
-                w_raw = wload.tile([P, T_PACK, R_POINTS, OUT], BF16)
-                for l in range(L_HALVES):
-                    nc.sync.dma_start(
-                        out=w_raw[l:P:L_HALVES].rearrange("q t r o -> q t (r o)"),
-                        in_=w_view[s, a, l],
-                    )
+        def if_how(i, how, stage):
+            if i < n_pass and passes[i][2] == how:
+                stage(i)
 
-                xq = xgrp.tile([P, B * T_PACK], BF16)
-                xq_words = xq[:].bitcast(F32).rearrange("p (b u) -> p b u", u=2)
-                for h in range(2):
-                    xt = xt_pool.tile([P, 2, 2 * P], F32)
-                    for u in range(2):
-                        for e in range(2):
-                            nc.tensor.transpose(
-                                xt[:, u, e * P : (e + 1) * P],
-                                x_twice[2 * h + e][
-                                    :, 2 * a + u, Q_CHUNKS * s : Q_CHUNKS * (s + 1), :
-                                ].rearrange("b q l -> b (q l)"),
-                                ident[:],
-                            )
-                    nc.scalar.copy(
-                        out=xq_words[:, 2 * P * h : 2 * P * (h + 1), :],
-                        in_=xt[:].rearrange("p u b -> p b u"),
-                    )
+        W_AHEAD = 4
+        V_AHEAD = 3
+        for i in range(V_AHEAD):
+            if_how(i, ON_VECTOR, exponent_on_vector)
+        for i in range(W_AHEAD):
+            group_w(i)
+            if i > 0:
+                quantise_w(i - 1)
+        if_how(0, MIXED, exponent_mixed)
 
-                for r in range(R_POINTS):
-                    w_grouped = work.tile([P, OUT, T_PACK], BF16, align_bytes=64)
-                    nc.vector.tensor_copy(
-                        out=w_grouped[:].rearrange("p (c i) t -> p c t i", i=4),
-                        in_=w_raw[:, :, r, :].rearrange("p t (c i) -> p c t i", i=4),
-                    )
-                    w_codes = work.tile([P, OUT], U32, align_bytes=64)
-                    w_scales = work.tile([P, OUT], U8, align_bytes=64)
-                    nc.vector.quantize_mx(
-                        out=w_codes[:].bitcast(FP8X4),
-                        scales=w_scales[:],
-                        in_=w_grouped[:].rearrange("p o t -> p (o t)"),
-                    )
+        for i in range(n_pass - 1):
+            if i % R_POINTS == 0 and i // R_POINTS + 2 < len(groups):
+                load_w(i // R_POINTS + 2)
+            quad, turn_now = (0, i == 0) if i < 4 else ((i + 4) // 8, i % 8 == 4)
+            turn_now = turn_now and quad < A_QUADS
+            if turn_now:
+                banks = turn_quad(quad)
+            if_how(i + 1, MIXED, exponent_mixed)
+            if_how(i + V_AHEAD, ON_VECTOR, exponent_on_vector)
+            if i + W_AHEAD < n_pass:
+                group_w(i + W_AHEAD)
+            if_how(i + 1, ON_SCALAR, exponent_on_scalar)
+            make_basis(i)
+            if turn_now:
+                spread_quad(quad, banks)
+            if i >= 1:
+                quantise_b(i - 1)
+            if i + W_AHEAD - 1 < n_pass:
+                quantise_w(i + W_AHEAD - 1)
+            if i >= 2:
+                multiply(i - 2)
 
-                    quad = work.tile([P, B * T_PACK], F32)
-                    basis = work.tile([P, B * T_PACK], BF16, align_bytes=64)
-                    if r % 2 == 0:
-                        nc.scalar.activation(
-                            out=quad[:], in_=xq[:], func=ACT.Square, bias=neg_g[:, r : r + 1], scale=1.0
-                        )
-                        nc.scalar.activation(out=basis[:], in_=quad[:], func=ACT.Exp, scale=-INV_H2)
-                    else:
-                        nc.vector.scalar_tensor_tensor(
-                            out=quad[:], in0=xq[:], scalar=two_g[:, r : r + 1], in1=xq[:],
-                            op0=ALU.subtract, op1=ALU.mult,
-                        )
-                        nc.scalar.activation(
-                            out=basis[:], in_=quad[:], func=ACT.Exp,
-                            bias=neg_g2_h2[:, r : r + 1], scale=-INV_H2,
-                        )
-                    b_codes = work.tile([P, B], U32, align_bytes=64)
-                    b_scales = work.tile([P, B], U8, align_bytes=64)
-                    nc.vector.quantize_mx(
-                        out=b_codes[:].bitcast(FP8X4), scales=b_scales[:], in_=basis[:]
-                    )
+        last = n_pass - 1
+        quantise_b(last - 1)
+        multiply(last - 2)
+        multiply(last - 1)
+        g_, r, how = passes[last]
+        basis[last] = work.tile([P, COLS], BF16, name="basis", align_bytes=64)
+        b_codes[last] = work.tile([P, B], U32, name="b_codes", bufs=5, align_bytes=64)
+        b_scales[last] = work.tile([P, B], U8, name="b_scales", bufs=5, align_bytes=64)
 
-                    for bt in range(B_TILES):
-                        b_cols = slice(bt * P, (bt + 1) * P)
-                        nc.tensor.matmul_mx(
-                            out=acc[bt][:],
-                            lhsT=b_codes[:, b_cols].bitcast(FP8X4),
-                            lhsT_scale=b_scales[:, b_cols],
-                            rhs=w_codes[:].bitcast(FP8X4),
-                            rhs_scale=w_scales[:],
-                            start=(i_pass == 0),
-                            stop=(i_pass == n_pass - 1),
-                        )
-                    i_pass += 1
-
-        for bt in range(B_TILES):
-            result = store.tile([P, OUT], F32)
-            if bt % 2 == 0:
+        def store_rows(bt):
+            result = store.tile([P, OUT], F32, name="result")
+            if bt < B_TILES - 1:
                 nc.vector.tensor_copy(out=result[:], in_=acc[bt][:])
             else:
                 nc.scalar.copy(out=result[:], in_=acc[bt][:])
             nc.sync.dma_start(out=out[bt * P : (bt + 1) * P, :], in_=result[:])
+
+        for bt in range(B_TILES):
+            b_cols = slice(bt * P, (bt + 1) * P)
+            cols = slice(bt * P * T_PACK, (bt + 1) * P * T_PACK)
+            nc.scalar.activation(
+                out=basis[last][:, cols], in_=mixed[last][bt][:], func=ACT.Exp,
+                bias=neg_g2_h2[:, r : r + 1], scale=-INV_H2,
+            )
+            nc.vector.quantize_mx(
+                out=b_codes[last][:, b_cols].bitcast(FP8X4), scales=b_scales[last][:, b_cols],
+                in_=basis[last][:, cols],
+            )
+            nc.tensor.matmul_mx(
+                out=acc[bt][:],
+                lhsT=b_codes[last][:, b_cols].bitcast(FP8X4), lhsT_scale=b_scales[last][:, b_cols],
+                rhs=w_codes[last][:].bitcast(FP8X4), rhs_scale=w_scales[last][:],
+                start=False, stop=True,
+            )
+            if bt > 0:
+                store_rows(bt - 1)
+        store_rows(B_TILES - 1)

@@ -21,27 +21,13 @@ INV_H2 = 49.0 / 16.0
 S_HALVES, Q_CHUNKS, A_QUADS, T_PACK, L_HALVES, R_POINTS = 2, 64, 4, 4, 2, 4
 B_TILES = B // P
 COLS = B * T_PACK
-
-ON_SCALAR, ON_VECTOR, MIXED = 0, 1, 2
+TILE_COLS = P * T_PACK
 
 
 def tile_gaussiankernel_k_kernel(tc, x, grid, spline_weight, out):
     nc = tc.nc
     groups = [(a, s) for a in range(A_QUADS) for s in range(S_HALVES)]
-    passes = []
-    for g in range(len(groups)):
-        if g % 2 == 0:
-            plan = [(3, ON_SCALAR), (1, MIXED), (0, ON_VECTOR), (2, MIXED)]
-        elif g < len(groups) - 1:
-            plan = [
-                (2, ON_SCALAR),
-                (0, ON_VECTOR),
-                (1, MIXED),
-                (3, ON_VECTOR if g % 4 == 1 else ON_SCALAR),
-            ]
-        else:
-            plan = [(2, ON_SCALAR), (0, ON_VECTOR), (3, ON_SCALAR), (1, MIXED)]
-        passes += [(g, r, how) for r, how in plan]
+    passes = [(g, r) for g in range(len(groups)) for r in range(R_POINTS)]
     n_pass = len(passes)
 
     with ExitStack() as ctx:
@@ -71,7 +57,7 @@ def tile_gaussiankernel_k_kernel(tc, x, grid, spline_weight, out):
                 )
 
         def load_w_pass(i):
-            g_, r, how = passes[i]
+            g_, r = passes[i]
             a, s = groups[g_]
             if g_ not in w_raw:
                 w_raw[g_] = wload.tile([P, T_PACK, R_POINTS, OUT], BF16, name="w_raw")
@@ -99,22 +85,12 @@ def tile_gaussiankernel_k_kernel(tc, x, grid, spline_weight, out):
 
         ident = const.tile([P, P], F32)
         make_identity(nc, ident[:])
-        g = const.tile([P, R_POINTS], F32)
-        nc.vector.tensor_copy(out=g[:], in_=g_bf[:])
-        neg_g = const.tile([P, R_POINTS], F32)
-        nc.vector.tensor_scalar_mul(out=neg_g[:], in0=g[:], scalar1=-1.0)
-        two_g = const.tile([P, R_POINTS], F32)
-        nc.vector.tensor_scalar_mul(out=two_g[:], in0=g[:], scalar1=2.0)
-        neg_g2_h2 = const.tile([P, R_POINTS], F32)
-        nc.vector.scalar_tensor_tensor(
-            out=neg_g2_h2[:], in0=g[:], scalar=-INV_H2, in1=g[:], op0=ALU.mult, op1=ALU.mult
-        )
-
         def words(bt, s):
             return x_rows[bt][:, s, :].bitcast(F32).rearrange("b (q c) -> b c q", c=8)
 
-        def turn_half(words_of, h):
-            bank = bank_pool.tile([P, 2, 2 * P], F32, name="bank")
+        def turn_half(words_of, h, bank=None):
+            if bank is None:
+                bank = bank_pool.tile([P, 2, 2 * P], F32, name="bank")
             for u in range(2):
                 for e in range(2):
                     nc.tensor.transpose(bank[:, u, e * P : (e + 1) * P], words_of(2 * h + e, u), ident[:])
@@ -135,7 +111,10 @@ def tile_gaussiankernel_k_kernel(tc, x, grid, spline_weight, out):
                     .rearrange("b (Q c) -> b c Q", c=8)[:, 2 * a + u, :]
                 )
 
-            return [turn_half(words_of, h) for h in range(2)]
+            return [
+                turn_half(words_of, h, acc_pool.tile([P, 2, 2 * P], F32, name="acc%d" % h) if a == 0 else None)
+                for h in range(2)
+            ]
 
         def spread_quad(a, banks):
             x_turned = work.tile([P, COLS], BF16, name="x_turned", bufs=2)
@@ -150,12 +129,12 @@ def tile_gaussiankernel_k_kernel(tc, x, grid, spline_weight, out):
                             in_=x_turned[Q_CHUNKS * s : Q_CHUNKS * (s + 1), :],
                         )
 
-        w_grouped, w_codes, w_scales, exponent, exponent_0, mixed, basis, b_codes, b_scales = (
+        w_grouped, w_codes, w_scales, exponent_0, exponent, mixed, basis, b_codes, b_scales = (
             {}, {}, {}, {}, {}, {}, {}, {}, {}
         )
 
         def group_w(i):
-            g_, r, how = passes[i]
+            g_, r = passes[i]
             w_grouped[i] = work.tile([P, OUT, T_PACK], BF16, name="w_grouped", bufs=3, align_bytes=64)
             nc.vector.tensor_copy(
                 out=w_grouped[i][:].rearrange("p (c i) t -> p c t i", i=4),
@@ -171,51 +150,63 @@ def tile_gaussiankernel_k_kernel(tc, x, grid, spline_weight, out):
                 in_=w_grouped[i][:].rearrange("p o t -> p (o t)"),
             )
 
-        def exponent_on_vector(i):
-            g_, r, how = passes[i]
-            name = "exponent_0" if r == 0 else "exponent"
-            exponent[i] = work.tile([P, COLS], F32, name=name, bufs=2 if r == 0 else 3)
-            if r == 0:
-                exponent_0[g_] = exponent[i]
+        def point_0_exponents(i, cols):
+            g_, r = passes[i]
+            if cols.start == 0:
+                exponent_0[g_] = work.tile([P, COLS], F32, name="exponent_0", bufs=2)
+            vector_exponents(exponent_0[g_][:, cols], g_, r, cols)
+
+        def vector_exponents(dst, g_, r, cols):
             nc.vector.scalar_tensor_tensor(
-                out=exponent[i][:], in0=xq[g_][:], scalar=two_g[:, r : r + 1], in1=xq[g_][:],
+                out=dst, in0=xq[g_][:, cols], scalar=two_g[:, r : r + 1], in1=xq[g_][:, cols],
                 op0=ALU.subtract, op1=ALU.mult,
             )
 
-        def exponent_on_scalar(i):
-            g_, r, how = passes[i]
-            exponent[i] = work.tile([P, COLS], F32, name="exponent", bufs=3)
-            nc.scalar.activation(
-                out=exponent[i][:], in_=xq[g_][:], func=ACT.Square, bias=neg_g[:, r : r + 1], scale=1.0
-            )
+        def on_vector(i):
+            g_, r = passes[i]
+            return r == 3 and g_ % 2 == 0
 
-        def exponent_mixed(i):
-            g_, r, how = passes[i]
-            mixed[i] = []
-            for bt in range(B_TILES):
-                bank = bank_pool.tile([P, P * T_PACK], F32, name="bank")
+        def first_rows_exponents(i):
+            g_, r = passes[i]
+            exponent[i] = work.tile([P, COLS // 2], F32, name="exponent")
+            cols = slice(0, COLS // 2)
+            if on_vector(i):
+                vector_exponents(exponent[i][:], g_, r, cols)
+            else:
+                nc.scalar.activation(
+                    out=exponent[i][:], in_=xq[g_][:, cols], func=ACT.Square, bias=neg_g[:, r : r + 1], scale=1.0
+                )
+
+        def last_rows_exponents(i):
+            g_, r = passes[i]
+            mixed[i] = {}
+            for bt in range(B_TILES // 2, B_TILES):
+                bank = bank_pool.tile([P, TILE_COLS], F32, name="bank")
                 nc.tensor.matmul(
-                    bank[:], lhsT=mix[r][:], rhs=exponent_0[g_][:, bt * P * T_PACK : (bt + 1) * P * T_PACK],
+                    bank[:], lhsT=mix[r][:], rhs=exponent_0[g_][:, bt * TILE_COLS : (bt + 1) * TILE_COLS],
                     start=True, stop=True,
                 )
-                mixed[i].append(bank)
+                mixed[i][bt] = bank
 
-        def make_basis(i):
-            g_, r, how = passes[i]
-            basis[i] = work.tile([P, COLS], BF16, name="basis", align_bytes=64)
-            if how == ON_SCALAR:
-                nc.scalar.activation(out=basis[i][:], in_=exponent[i][:], func=ACT.Exp, scale=-INV_H2)
-            elif how == ON_VECTOR:
+        def exp(i, cols, source, has_g2):
+            g_, r = passes[i]
+            if has_g2:
+                nc.scalar.activation(out=basis[i][:, cols], in_=source, func=ACT.Exp, scale=-INV_H2)
+            else:
                 nc.scalar.activation(
-                    out=basis[i][:], in_=exponent[i][:], func=ACT.Exp,
+                    out=basis[i][:, cols], in_=source, func=ACT.Exp,
                     bias=neg_g2_h2[:, r : r + 1], scale=-INV_H2,
                 )
+
+        def make_basis(i):
+            g_, r = passes[i]
+            basis[i] = work.tile([P, COLS], BF16, name="basis", align_bytes=64)
+            if r == 0:
+                exp(i, slice(0, COLS), exponent_0[g_][:], False)
             else:
-                for bt in range(B_TILES):
-                    nc.scalar.activation(
-                        out=basis[i][:, bt * P * T_PACK : (bt + 1) * P * T_PACK], in_=mixed[i][bt][:],
-                        func=ACT.Exp, bias=neg_g2_h2[:, r : r + 1], scale=-INV_H2,
-                    )
+                exp(i, slice(0, COLS // 2), exponent[i][:], not on_vector(i))
+                for bt in range(B_TILES // 2, B_TILES):
+                    exp(i, slice(bt * TILE_COLS, (bt + 1) * TILE_COLS), mixed[i][bt][:], False)
 
         def quantise_b(i):
             b_codes[i] = work.tile([P, B], U32, name="b_codes", bufs=5, align_bytes=64)
@@ -224,7 +215,7 @@ def tile_gaussiankernel_k_kernel(tc, x, grid, spline_weight, out):
                 out=b_codes[i][:].bitcast(FP8X4), scales=b_scales[i][:], in_=basis[i][:]
             )
 
-        acc = [acc_pool.tile([P, OUT], F32, name="acc%d" % bt) for bt in range(B_TILES)]
+        acc = []
 
         def multiply(i):
             for bt in range(B_TILES):
@@ -239,27 +230,33 @@ def tile_gaussiankernel_k_kernel(tc, x, grid, spline_weight, out):
                     stop=False,
                 )
 
+        x_twice = []
+        for bt in range(B_TILES):
+            twice = xin.tile([P, 2, Q_CHUNKS, L_HALVES], F32, name="twice")
+            nc.vector.tensor_copy(
+                out=twice[:],
+                in_=words(bt, 0)[:, 0:2, :].unsqueeze(3).to_broadcast([P, 2, Q_CHUNKS, L_HALVES]),
+            )
+            x_twice.append(twice)
+        g = const.tile([P, R_POINTS], F32)
+        nc.vector.tensor_copy(out=g[:], in_=g_bf[:])
+        neg_g = const.tile([P, R_POINTS], F32)
+        nc.vector.tensor_scalar_mul(out=neg_g[:], in0=g[:], scalar1=-1.0)
+        two_g = const.tile([P, R_POINTS], F32)
+        nc.vector.tensor_scalar_mul(out=two_g[:], in0=g[:], scalar1=2.0)
+        neg_g2_h2 = const.tile([P, R_POINTS], F32)
+        nc.vector.scalar_tensor_tensor(
+            out=neg_g2_h2[:], in0=g[:], scalar=-INV_H2, in1=g[:], op0=ALU.mult, op1=ALU.mult
+        )
+
         for h in range(2):
-            x_twice = []
-            for bt in (2 * h, 2 * h + 1):
-                twice = xin.tile([P, 2, Q_CHUNKS, L_HALVES], F32, name="twice")
-                nc.vector.tensor_copy(
-                    out=twice[:],
-                    in_=words(bt, 0)[:, 0:2, :].unsqueeze(3).to_broadcast([P, 2, Q_CHUNKS, L_HALVES]),
-                )
-                x_twice.append(twice)
-            copy_half(
-                xq[0],
-                turn_half(lambda bt, u: x_twice[bt - 2 * h][:, u].rearrange("b q l -> b (q l)"), h),
-                h,
-            )
-            cols = slice(h * COLS // 2, (h + 1) * COLS // 2)
+            bank = turn_half(lambda bt, u: x_twice[bt][:, u].rearrange("b q l -> b (q l)"), h)
+            copy_half(xq[0], bank, h)
             if h == 0:
-                exponent[0] = work.tile([P, COLS], F32, name="exponent", bufs=3)
-            nc.scalar.activation(
-                out=exponent[0][:, cols], in_=xq[0][:, cols], func=ACT.Square,
-                bias=neg_g[:, passes[0][1] : passes[0][1] + 1], scale=1.0,
-            )
+                first_rows_exponents(1)
+        point_0_exponents(0, slice(0, COLS // 2))
+        point_0_exponents(0, slice(COLS // 2, COLS))
+        first_rows_exponents(2)
 
         g_all = const.tile([P, G], F32)
         nc.vector.tensor_copy(out=g_all[:], in_=g_all_bf[:])
@@ -284,7 +281,7 @@ def tile_gaussiankernel_k_kernel(tc, x, grid, spline_weight, out):
         same_q = const.tile([P, Q_CHUNKS], F32)
         nc.vector.tensor_add(out=same_q[:], in0=ident_ql[:, :, 0], in1=ident_ql[:, :, 1])
         mix = {}
-        for r in (1, 2):
+        for r in range(1, R_POINTS):
             mix[r] = const.tile([P, P], F32, name="mix%d" % r)
             for l in range(L_HALVES):
                 j = R_POINTS * l + r
@@ -293,47 +290,53 @@ def tile_gaussiankernel_k_kernel(tc, x, grid, spline_weight, out):
                     in0=same_q[:], scalar1=weight[:, j : j + 1],
                 )
 
-        def if_how(i, how, stage):
-            if i < n_pass and passes[i][2] == how:
-                stage(i)
-
         W_AHEAD = 4
-        V_AHEAD = 3
-        for i in range(V_AHEAD):
-            if_how(i, ON_VECTOR, exponent_on_vector)
+        POINT_0_AHEAD = 3
+        VECTOR_AHEAD = 3
+        SCALAR_AHEAD = 2
+        MIX_AHEAD = 2
         for i in range(W_AHEAD):
             group_w(i)
             if i > 0:
                 quantise_w(i - 1)
-        if_how(0, MIXED, exponent_mixed)
-
+        first_rows_exponents(3)
+        last_rows_exponents(1)
         for i in range(n_pass - 1):
-            if i % R_POINTS == 0 and i // R_POINTS + 2 < len(groups):
-                load_w(i // R_POINTS + 2)
-            quad, turn_now = (0, i == 0) if i < 4 else ((i + 4) // 8, i % 8 == 4)
-            turn_now = turn_now and quad < A_QUADS
-            if turn_now:
+            g_, r = passes[i]
+            if r == 0 and g_ + 2 < len(groups):
+                load_w(g_ + 2)
+            if i + MIX_AHEAD < n_pass and passes[i + MIX_AHEAD][1] > 0:
+                last_rows_exponents(i + MIX_AHEAD)
+            quad = 0 if i == 0 else i // 8 + 1 if i % 8 == 2 else A_QUADS
+            if quad < A_QUADS:
                 banks = turn_quad(quad)
-            if_how(i + 1, MIXED, exponent_mixed)
-            if_how(i + V_AHEAD, ON_VECTOR, exponent_on_vector)
+            ahead = i + POINT_0_AHEAD
+            if ahead < n_pass and passes[ahead][1] == 0:
+                point_0_exponents(ahead, slice(0, COLS))
+            ahead = i + VECTOR_AHEAD
+            if 3 < ahead < n_pass and passes[ahead][1] > 0 and on_vector(ahead):
+                first_rows_exponents(ahead)
             if i + W_AHEAD < n_pass:
                 group_w(i + W_AHEAD)
-            if_how(i + 1, ON_SCALAR, exponent_on_scalar)
+            ahead = i + SCALAR_AHEAD
+            if 3 < ahead < n_pass and passes[ahead][1] > 0 and not on_vector(ahead):
+                first_rows_exponents(ahead)
             make_basis(i)
-            if turn_now:
+            if quad < A_QUADS:
                 spread_quad(quad, banks)
+            if i == 0:
+                acc += [acc_pool.tile([P, OUT], F32, name="acc%d" % bt) for bt in range(B_TILES)]
             if i >= 1:
                 quantise_b(i - 1)
             if i + W_AHEAD - 1 < n_pass:
                 quantise_w(i + W_AHEAD - 1)
-            if i >= 2:
-                multiply(i - 2)
+            if i >= 3:
+                multiply(i - 3)
 
         last = n_pass - 1
         quantise_b(last - 1)
-        multiply(last - 2)
-        multiply(last - 1)
-        g_, r, how = passes[last]
+        for i in range(last - 3, last):
+            multiply(i)
         basis[last] = work.tile([P, COLS], BF16, name="basis", align_bytes=64)
         b_codes[last] = work.tile([P, B], U32, name="b_codes", bufs=5, align_bytes=64)
         b_scales[last] = work.tile([P, B], U8, name="b_scales", bufs=5, align_bytes=64)
@@ -348,11 +351,11 @@ def tile_gaussiankernel_k_kernel(tc, x, grid, spline_weight, out):
 
         for bt in range(B_TILES):
             b_cols = slice(bt * P, (bt + 1) * P)
-            cols = slice(bt * P * T_PACK, (bt + 1) * P * T_PACK)
-            nc.scalar.activation(
-                out=basis[last][:, cols], in_=mixed[last][bt][:], func=ACT.Exp,
-                bias=neg_g2_h2[:, r : r + 1], scale=-INV_H2,
-            )
+            cols = slice(bt * TILE_COLS, (bt + 1) * TILE_COLS)
+            if bt < B_TILES // 2:
+                exp(last, cols, exponent[last][:, cols], not on_vector(last))
+            else:
+                exp(last, cols, mixed[last][bt][:], False)
             nc.vector.quantize_mx(
                 out=b_codes[last][:, b_cols].bitcast(FP8X4), scales=b_scales[last][:, b_cols],
                 in_=basis[last][:, cols],

@@ -27,8 +27,16 @@ TILE_COLS = P * T_PACK
 def tile_gaussiankernel_k_kernel(tc, x, grid, spline_weight, out):
     nc = tc.nc
     groups = [(a, s) for a in range(A_QUADS) for s in range(S_HALVES)]
-    passes = [(g, r) for g in range(len(groups)) for r in range(R_POINTS)]
+    passes = [(g, r) for g in range(len(groups)) for r in (0, 3, 1, 2)]
     n_pass = len(passes)
+
+    def plan(i):
+        g_, r = passes[i]
+        if r == 0:
+            return B_TILES, B_TILES
+        if r == 3:
+            return 1 + g_ % 2, B_TILES - 1
+        return 0, B_TILES - 2
 
     with ExitStack() as ctx:
         const = ctx.enter_context(tc.tile_pool(name="const", bufs=1))
@@ -129,9 +137,8 @@ def tile_gaussiankernel_k_kernel(tc, x, grid, spline_weight, out):
                             in_=x_turned[Q_CHUNKS * s : Q_CHUNKS * (s + 1), :],
                         )
 
-        w_grouped, w_codes, w_scales, exponent_0, exponent, mixed, basis, b_codes, b_scales = (
-            {}, {}, {}, {}, {}, {}, {}, {}, {}
-        )
+        w_grouped, w_codes, w_scales, basis, b_codes, b_scales = {}, {}, {}, {}, {}, {}
+        exponent_0, on_vector, on_scalar, mixed = {}, {}, {}, {}
 
         def group_w(i):
             g_, r = passes[i]
@@ -150,37 +157,38 @@ def tile_gaussiankernel_k_kernel(tc, x, grid, spline_weight, out):
                 in_=w_grouped[i][:].rearrange("p o t -> p (o t)"),
             )
 
-        def point_0_exponents(i, cols):
+        def vector_exponents(i):
             g_, r = passes[i]
-            if cols.start == 0:
+            v, m = plan(i)
+            if v == 0:
+                return
+            if r == 0:
                 exponent_0[g_] = work.tile([P, COLS], F32, name="exponent_0", bufs=2)
-            vector_exponents(exponent_0[g_][:, cols], g_, r, cols)
-
-        def vector_exponents(dst, g_, r, cols):
+                on_vector[i] = exponent_0[g_]
+            else:
+                on_vector[i] = work.tile([P, COLS // 2], F32, name="on_vector", bufs=3)
+            cols = slice(0, v * TILE_COLS)
             nc.vector.scalar_tensor_tensor(
-                out=dst, in0=xq[g_][:, cols], scalar=two_g[:, r : r + 1], in1=xq[g_][:, cols],
+                out=on_vector[i][:, cols], in0=xq[g_][:, cols], scalar=two_g[:, r : r + 1], in1=xq[g_][:, cols],
                 op0=ALU.subtract, op1=ALU.mult,
             )
 
-        def on_vector(i):
+        def scalar_exponents(i):
             g_, r = passes[i]
-            return r == 3 and g_ % 2 == 0
+            v, m = plan(i)
+            if m == v:
+                return
+            on_scalar[i] = work.tile([P, COLS // 2], F32, name="on_scalar", bufs=3)
+            nc.scalar.activation(
+                out=on_scalar[i][:, : (m - v) * TILE_COLS], in_=xq[g_][:, v * TILE_COLS : m * TILE_COLS],
+                func=ACT.Square, bias=neg_g[:, r : r + 1], scale=1.0,
+            )
 
-        def first_rows_exponents(i):
+        def mixed_exponents(i):
             g_, r = passes[i]
-            exponent[i] = work.tile([P, COLS // 2], F32, name="exponent")
-            cols = slice(0, COLS // 2)
-            if on_vector(i):
-                vector_exponents(exponent[i][:], g_, r, cols)
-            else:
-                nc.scalar.activation(
-                    out=exponent[i][:], in_=xq[g_][:, cols], func=ACT.Square, bias=neg_g[:, r : r + 1], scale=1.0
-                )
-
-        def last_rows_exponents(i):
-            g_, r = passes[i]
+            v, m = plan(i)
             mixed[i] = {}
-            for bt in range(B_TILES // 2, B_TILES):
+            for bt in range(m, B_TILES):
                 bank = bank_pool.tile([P, TILE_COLS], F32, name="bank")
                 nc.tensor.matmul(
                     bank[:], lhsT=mix[r][:], rhs=exponent_0[g_][:, bt * TILE_COLS : (bt + 1) * TILE_COLS],
@@ -188,25 +196,26 @@ def tile_gaussiankernel_k_kernel(tc, x, grid, spline_weight, out):
                 )
                 mixed[i][bt] = bank
 
-        def exp(i, cols, source, has_g2):
+        def make_basis(i, first=0, end=B_TILES):
             g_, r = passes[i]
-            if has_g2:
-                nc.scalar.activation(out=basis[i][:, cols], in_=source, func=ACT.Exp, scale=-INV_H2)
-            else:
+            v, m = plan(i)
+            if first == 0:
+                basis[i] = work.tile([P, COLS], BF16, name="basis", align_bytes=64)
+
+            def exp(t0, t1, source, bias):
                 nc.scalar.activation(
-                    out=basis[i][:, cols], in_=source, func=ACT.Exp,
-                    bias=neg_g2_h2[:, r : r + 1], scale=-INV_H2,
+                    out=basis[i][:, t0 * TILE_COLS : t1 * TILE_COLS], in_=source,
+                    func=ACT.Exp, bias=bias, scale=-INV_H2,
                 )
 
-        def make_basis(i):
-            g_, r = passes[i]
-            basis[i] = work.tile([P, COLS], BF16, name="basis", align_bytes=64)
-            if r == 0:
-                exp(i, slice(0, COLS), exponent_0[g_][:], False)
-            else:
-                exp(i, slice(0, COLS // 2), exponent[i][:], not on_vector(i))
-                for bt in range(B_TILES // 2, B_TILES):
-                    exp(i, slice(bt * TILE_COLS, (bt + 1) * TILE_COLS), mixed[i][bt][:], False)
+            t0, t1 = first, min(v, end)
+            if t0 < t1:
+                exp(t0, t1, on_vector[i][:, t0 * TILE_COLS : t1 * TILE_COLS], neg_g2_h2[:, r : r + 1])
+            t0, t1 = max(v, first), min(m, end)
+            if t0 < t1:
+                exp(t0, t1, on_scalar[i][:, (t0 - v) * TILE_COLS : (t1 - v) * TILE_COLS], 0.0)
+            for bt in range(max(m, first), end):
+                exp(bt, bt + 1, mixed[i][bt][:], neg_g2_h2[:, r : r + 1])
 
         def quantise_b(i):
             b_codes[i] = work.tile([P, B], U32, name="b_codes", bufs=5, align_bytes=64)
@@ -252,12 +261,6 @@ def tile_gaussiankernel_k_kernel(tc, x, grid, spline_weight, out):
         for h in range(2):
             bank = turn_half(lambda bt, u: x_twice[bt][:, u].rearrange("b q l -> b (q l)"), h)
             copy_half(xq[0], bank, h)
-            if h == 0:
-                first_rows_exponents(1)
-        point_0_exponents(0, slice(0, COLS // 2))
-        point_0_exponents(0, slice(COLS // 2, COLS))
-        first_rows_exponents(2)
-
         g_all = const.tile([P, G], F32)
         nc.vector.tensor_copy(out=g_all[:], in_=g_all_bf[:])
         share = const.tile([P, G], F32)
@@ -290,60 +293,65 @@ def tile_gaussiankernel_k_kernel(tc, x, grid, spline_weight, out):
                     in0=same_q[:], scalar1=weight[:, j : j + 1],
                 )
 
+        vector_exponents(0)
+        scalar_exponents(1)
+        scalar_exponents(2)
+
         W_AHEAD = 4
-        POINT_0_AHEAD = 3
         VECTOR_AHEAD = 3
         SCALAR_AHEAD = 2
         MIX_AHEAD = 2
+        MULTIPLY_BEHIND = 3
+        for i in range(1, VECTOR_AHEAD):
+            vector_exponents(i)
         for i in range(W_AHEAD):
             group_w(i)
             if i > 0:
                 quantise_w(i - 1)
-        first_rows_exponents(3)
-        last_rows_exponents(1)
+        banks = turn_quad(0)
+        for i in range(1, MIX_AHEAD):
+            mixed_exponents(i)
         for i in range(n_pass - 1):
-            g_, r = passes[i]
-            if r == 0 and g_ + 2 < len(groups):
-                load_w(g_ + 2)
-            if i + MIX_AHEAD < n_pass and passes[i + MIX_AHEAD][1] > 0:
-                last_rows_exponents(i + MIX_AHEAD)
-            quad = 0 if i == 0 else i // 8 + 1 if i % 8 == 2 else A_QUADS
-            if quad < A_QUADS:
+            g_ = passes[i][0]
+            quad = 0 if i == 0 else i // 8 + 1 if i % 8 == 3 else A_QUADS
+            if 0 < quad < A_QUADS:
                 banks = turn_quad(quad)
-            ahead = i + POINT_0_AHEAD
-            if ahead < n_pass and passes[ahead][1] == 0:
-                point_0_exponents(ahead, slice(0, COLS))
-            ahead = i + VECTOR_AHEAD
-            if 3 < ahead < n_pass and passes[ahead][1] > 0 and on_vector(ahead):
-                first_rows_exponents(ahead)
+            if i >= n_pass - R_POINTS:
+                multiply(i - 2)
+            if i + MIX_AHEAD < n_pass:
+                mixed_exponents(i + MIX_AHEAD)
+            if MULTIPLY_BEHIND <= i < n_pass - R_POINTS:
+                multiply(i - MULTIPLY_BEHIND)
+            if i + VECTOR_AHEAD < n_pass:
+                vector_exponents(i + VECTOR_AHEAD)
             if i + W_AHEAD < n_pass:
                 group_w(i + W_AHEAD)
-            ahead = i + SCALAR_AHEAD
-            if 3 < ahead < n_pass and passes[ahead][1] > 0 and not on_vector(ahead):
-                first_rows_exponents(ahead)
+            if 2 < i + SCALAR_AHEAD < n_pass:
+                scalar_exponents(i + SCALAR_AHEAD)
             make_basis(i)
             if quad < A_QUADS:
                 spread_quad(quad, banks)
+            if i % R_POINTS == 0 and g_ + 2 < len(groups):
+                load_w(g_ + 2)
             if i == 0:
                 acc += [acc_pool.tile([P, OUT], F32, name="acc%d" % bt) for bt in range(B_TILES)]
             if i >= 1:
                 quantise_b(i - 1)
+            if i == n_pass - R_POINTS - 1:
+                multiply(i - 2)
             if i + W_AHEAD - 1 < n_pass:
                 quantise_w(i + W_AHEAD - 1)
-            if i >= 3:
-                multiply(i - 3)
 
         last = n_pass - 1
+        multiply(last - 2)
         quantise_b(last - 1)
-        for i in range(last - 3, last):
-            multiply(i)
-        basis[last] = work.tile([P, COLS], BF16, name="basis", align_bytes=64)
+        multiply(last - 1)
         b_codes[last] = work.tile([P, B], U32, name="b_codes", bufs=5, align_bytes=64)
         b_scales[last] = work.tile([P, B], U8, name="b_scales", bufs=5, align_bytes=64)
 
         def store_rows(bt):
             result = store.tile([P, OUT], F32, name="result")
-            if bt < B_TILES - 1:
+            if bt % 2 == 0:
                 nc.vector.tensor_copy(out=result[:], in_=acc[bt][:])
             else:
                 nc.scalar.copy(out=result[:], in_=acc[bt][:])
@@ -352,10 +360,7 @@ def tile_gaussiankernel_k_kernel(tc, x, grid, spline_weight, out):
         for bt in range(B_TILES):
             b_cols = slice(bt * P, (bt + 1) * P)
             cols = slice(bt * TILE_COLS, (bt + 1) * TILE_COLS)
-            if bt < B_TILES // 2:
-                exp(last, cols, exponent[last][:, cols], not on_vector(last))
-            else:
-                exp(last, cols, mixed[last][bt][:], False)
+            make_basis(last, bt, bt + 1)
             nc.vector.quantize_mx(
                 out=b_codes[last][:, b_cols].bitcast(FP8X4), scales=b_scales[last][:, b_cols],
                 in_=basis[last][:, cols],

@@ -27,7 +27,7 @@ TILE_COLS = P * T_PACK
 def tile_gaussiankernel_k_kernel(tc, x, grid, spline_weight, out):
     nc = tc.nc
     groups = [(a, s) for a in range(A_QUADS) for s in range(S_HALVES)]
-    passes = [(g, r) for g in range(len(groups)) for r in (0, 3, 1, 2)]
+    passes = [(g, r) for g in range(len(groups)) for r in (0, 1, 3, 2)]
     n_pass = len(passes)
 
     def plan(i):
@@ -35,7 +35,7 @@ def tile_gaussiankernel_k_kernel(tc, x, grid, spline_weight, out):
         if r == 0:
             return B_TILES, B_TILES
         if r == 3:
-            return 1 + g_ % 2, B_TILES - 1
+            return 2, B_TILES
         return 0, B_TILES - 2
 
     with ExitStack() as ctx:
@@ -284,7 +284,7 @@ def tile_gaussiankernel_k_kernel(tc, x, grid, spline_weight, out):
         same_q = const.tile([P, Q_CHUNKS], F32)
         nc.vector.tensor_add(out=same_q[:], in0=ident_ql[:, :, 0], in1=ident_ql[:, :, 1])
         mix = {}
-        for r in range(1, R_POINTS):
+        for r in (1, 2):
             mix[r] = const.tile([P, P], F32, name="mix%d" % r)
             for l in range(L_HALVES):
                 j = R_POINTS * l + r
@@ -313,7 +313,7 @@ def tile_gaussiankernel_k_kernel(tc, x, grid, spline_weight, out):
             mixed_exponents(i)
         for i in range(n_pass - 1):
             g_ = passes[i][0]
-            quad = 0 if i == 0 else i // 8 + 1 if i % 8 == 3 else A_QUADS
+            quad = 0 if i == 0 else i // 8 + 1 if i % 8 == 2 else A_QUADS
             if 0 < quad < A_QUADS:
                 banks = turn_quad(quad)
             if i >= n_pass - R_POINTS:

@@ -34,8 +34,10 @@ def tile_gaussiankernel_k_kernel(tc, x, grid, spline_weight, out):
         g_, r = passes[i]
         if r == 0:
             return B_TILES, B_TILES
-        if r == 3:
+        if g_ == len(groups) - 1:
             return 2, B_TILES
+        if r == 3:
+            return 2, B_TILES - 1 if g_ < len(groups) // 2 else B_TILES
         return 0, B_TILES - 2
 
     with ExitStack() as ctx:
@@ -72,14 +74,11 @@ def tile_gaussiankernel_k_kernel(tc, x, grid, spline_weight, out):
             for l in range(L_HALVES):
                 nc.sync.dma_start(out=w_raw[g_][l:P:L_HALVES, :, r, :], in_=w_view[s, a, l, :, :, r, :])
 
-        g_bf = const.tile([P, R_POINTS], BF16)
-        for l in range(L_HALVES):
-            nc.scalar.dma_start(
-                out=g_bf[l:P:L_HALVES, :],
-                in_=grid[R_POINTS * l : R_POINTS * (l + 1)].partition_broadcast(Q_CHUNKS),
-            )
-        g_all_bf = const.tile([P, G], BF16)
-        nc.scalar.dma_start(out=g_all_bf[:], in_=grid.partition_broadcast(P))
+        grid_row = const.tile([P, G], BF16)
+        nc.vector.memset(grid_row[:], 0.0)
+        nc.sync.dma_start(out=grid_row[0:1, :], in_=grid.unsqueeze(0))
+        ones = const.tile([P, P], BF16)
+        nc.gpsimd.memset(ones[:], 1.0)
         x_rows = [xin.tile([P, S_HALVES, IN // S_HALVES], BF16, name="x_rows") for bt in range(B_TILES)]
         for s in range(S_HALVES):
             for bt in range(B_TILES):
@@ -93,6 +92,19 @@ def tile_gaussiankernel_k_kernel(tc, x, grid, spline_weight, out):
 
         ident = const.tile([P, P], F32)
         make_identity(nc, ident[:])
+        ident_ql = ident[:].rearrange("p (q l) -> p q l", l=L_HALVES)
+        odd = const.tile([P, 1], F32)
+        nc.vector.reduce_sum(out=odd[:], in_=ident_ql[:, :, 1], axis=AX.X)
+        even = const.tile([P, 1], F32)
+        nc.vector.tensor_scalar(out=even[:], in0=odd[:], scalar1=-1.0, scalar2=1.0, op0=ALU.mult, op1=ALU.add)
+        sign = const.tile([P, 1], F32)
+        nc.vector.tensor_sub(out=sign[:], in0=odd[:], in1=even[:])
+        same_q = const.tile([P, Q_CHUNKS], F32)
+        nc.vector.tensor_add(out=same_q[:], in0=ident_ql[:, :, 0], in1=ident_ql[:, :, 1])
+
+        grid_bank = acc_pool.tile([P, G], F32, name="acc3")
+        nc.tensor.matmul(grid_bank[:], lhsT=ones[:], rhs=grid_row[:], start=True, stop=True)
+
         def words(bt, s):
             return x_rows[bt][:, s, :].bitcast(F32).rearrange("b (q c) -> b c q", c=8)
 
@@ -247,8 +259,14 @@ def tile_gaussiankernel_k_kernel(tc, x, grid, spline_weight, out):
                 in_=words(bt, 0)[:, 0:2, :].unsqueeze(3).to_broadcast([P, 2, Q_CHUNKS, L_HALVES]),
             )
             x_twice.append(twice)
+        g_all = const.tile([P, G], F32)
+        nc.vector.tensor_copy(out=g_all[:], in_=grid_bank[:])
+        g_odd = const.tile([P, R_POINTS], F32)
+        nc.vector.tensor_scalar_mul(out=g_odd[:], in0=g_all[:, R_POINTS:], scalar1=odd[:])
         g = const.tile([P, R_POINTS], F32)
-        nc.vector.tensor_copy(out=g[:], in_=g_bf[:])
+        nc.vector.scalar_tensor_tensor(
+            out=g[:], in0=g_all[:, :R_POINTS], scalar=even[:], in1=g_odd[:], op0=ALU.mult, op1=ALU.add
+        )
         neg_g = const.tile([P, R_POINTS], F32)
         nc.vector.tensor_scalar_mul(out=neg_g[:], in0=g[:], scalar1=-1.0)
         two_g = const.tile([P, R_POINTS], F32)
@@ -261,8 +279,6 @@ def tile_gaussiankernel_k_kernel(tc, x, grid, spline_weight, out):
         for h in range(2):
             bank = turn_half(lambda bt, u: x_twice[bt][:, u].rearrange("b q l -> b (q l)"), h)
             copy_half(xq[0], bank, h)
-        g_all = const.tile([P, G], F32)
-        nc.vector.tensor_copy(out=g_all[:], in_=g_all_bf[:])
         share = const.tile([P, G], F32)
         nc.vector.tensor_scalar(
             out=share[:], in0=g_all[:], scalar1=g_all[:, 0:1], scalar2=None, op0=ALU.subtract
@@ -270,21 +286,12 @@ def tile_gaussiankernel_k_kernel(tc, x, grid, spline_weight, out):
         inv_span = const.tile([P, 1], F32)
         nc.vector.reciprocal(out=inv_span[:], in_=share[:, R_POINTS : R_POINTS + 1])
         nc.vector.tensor_scalar_mul(out=share[:], in0=share[:], scalar1=inv_span[:])
-        ident_ql = ident[:].rearrange("p (q l) -> p q l", l=L_HALVES)
-        odd = const.tile([P, 1], F32)
-        nc.vector.reduce_sum(out=odd[:], in_=ident_ql[:, :, 1], axis=AX.X)
-        sign = const.tile([P, 1], F32)
-        nc.vector.tensor_scalar(out=sign[:], in0=odd[:], scalar1=2.0, scalar2=-1.0, op0=ALU.mult, op1=ALU.add)
-        even = const.tile([P, 1], F32)
-        nc.vector.tensor_scalar(out=even[:], in0=odd[:], scalar1=-1.0, scalar2=1.0, op0=ALU.mult, op1=ALU.add)
         weight = const.tile([P, G], F32)
         nc.vector.tensor_scalar(
             out=weight[:], in0=share[:], scalar1=sign[:], scalar2=even[:], op0=ALU.mult, op1=ALU.add
         )
-        same_q = const.tile([P, Q_CHUNKS], F32)
-        nc.vector.tensor_add(out=same_q[:], in0=ident_ql[:, :, 0], in1=ident_ql[:, :, 1])
         mix = {}
-        for r in (1, 2):
+        for r in range(1, R_POINTS):
             mix[r] = const.tile([P, P], F32, name="mix%d" % r)
             for l in range(L_HALVES):
                 j = R_POINTS * l + r
@@ -301,7 +308,7 @@ def tile_gaussiankernel_k_kernel(tc, x, grid, spline_weight, out):
         VECTOR_AHEAD = 3
         SCALAR_AHEAD = 2
         MIX_AHEAD = 2
-        MULTIPLY_BEHIND = 3
+        MULTIPLY_BEHIND = 2
         for i in range(1, VECTOR_AHEAD):
             vector_exponents(i)
         for i in range(W_AHEAD):
@@ -316,11 +323,9 @@ def tile_gaussiankernel_k_kernel(tc, x, grid, spline_weight, out):
             quad = 0 if i == 0 else i // 8 + 1 if i % 8 == 2 else A_QUADS
             if 0 < quad < A_QUADS:
                 banks = turn_quad(quad)
-            if i >= n_pass - R_POINTS:
-                multiply(i - 2)
             if i + MIX_AHEAD < n_pass:
                 mixed_exponents(i + MIX_AHEAD)
-            if MULTIPLY_BEHIND <= i < n_pass - R_POINTS:
+            if i >= MULTIPLY_BEHIND:
                 multiply(i - MULTIPLY_BEHIND)
             if i + VECTOR_AHEAD < n_pass:
                 vector_exponents(i + VECTOR_AHEAD)
@@ -337,8 +342,6 @@ def tile_gaussiankernel_k_kernel(tc, x, grid, spline_weight, out):
                 acc += [acc_pool.tile([P, OUT], F32, name="acc%d" % bt) for bt in range(B_TILES)]
             if i >= 1:
                 quantise_b(i - 1)
-            if i == n_pass - R_POINTS - 1:
-                multiply(i - 2)
             if i + W_AHEAD - 1 < n_pass:
                 quantise_w(i + W_AHEAD - 1)
 

@@ -132,12 +132,12 @@ def tile_gaussiankernel_k_kernel(tc, x, grid, spline_weight, out):
                 )
 
             return [
-                turn_half(words_of, h, acc_pool.tile([P, 2, 2 * P], F32, name="acc%d" % h) if a == 0 else None)
+                turn_half(words_of, h, acc_pool.tile([P, 2, 2 * P], F32, name="acc%d" % (2 * (a % 2) + h)))
                 for h in range(2)
             ]
 
         def spread_quad(a, banks):
-            x_turned = work.tile([P, COLS], BF16, name="x_turned", bufs=2)
+            x_turned = work.tile([P, COLS], BF16, name="x_turned")
             for h in range(2):
                 copy_half(x_turned, banks[h], h)
             for g_ in range(len(groups)):
@@ -154,20 +154,23 @@ def tile_gaussiankernel_k_kernel(tc, x, grid, spline_weight, out):
 
         def group_w(i):
             g_, r = passes[i]
-            w_grouped[i] = work.tile([P, OUT, T_PACK], BF16, name="w_grouped", bufs=3, align_bytes=64)
+            if i % 2 == 0:
+                w_grouped[i] = work.tile([P, 2, OUT, T_PACK], BF16, name="w_grouped", bufs=2, align_bytes=64)
             nc.vector.tensor_copy(
-                out=w_grouped[i][:].rearrange("p (c i) t -> p c t i", i=4),
+                out=w_grouped[i - i % 2][:, i % 2].rearrange("p (c i) t -> p c t i", i=4),
                 in_=w_raw[g_][:, :, r, :].rearrange("p t (c i) -> p c t i", i=4),
             )
 
-        def quantise_w(i):
-            w_codes[i] = work.tile([P, OUT], U32, name="w_codes", bufs=7, align_bytes=64)
-            w_scales[i] = work.tile([P, OUT], U8, name="w_scales", bufs=7, align_bytes=64)
+        def quantise_w_pair(i):
+            codes = work.tile([P, 2, OUT], U32, name="w_codes", align_bytes=64)
+            scales = work.tile([P, 2, OUT], U8, name="w_scales", align_bytes=64)
             nc.vector.quantize_mx(
-                out=w_codes[i][:].bitcast(FP8X4),
-                scales=w_scales[i][:],
-                in_=w_grouped[i][:].rearrange("p o t -> p (o t)"),
+                out=codes[:].rearrange("p j o -> p (j o)").bitcast(FP8X4),
+                scales=scales[:].rearrange("p j o -> p (j o)"),
+                in_=w_grouped[i][:].rearrange("p j o t -> p (j o t)"),
             )
+            for j in range(2):
+                w_codes[i + j], w_scales[i + j] = codes[:, j], scales[:, j]
 
         def vector_exponents(i):
             g_, r = passes[i]
@@ -245,8 +248,8 @@ def tile_gaussiankernel_k_kernel(tc, x, grid, spline_weight, out):
                     out=acc[bt][:],
                     lhsT=b_codes[i][:, b_cols].bitcast(FP8X4),
                     lhsT_scale=b_scales[i][:, b_cols],
-                    rhs=w_codes[i][:].bitcast(FP8X4),
-                    rhs_scale=w_scales[i][:],
+                    rhs=w_codes[i].bitcast(FP8X4),
+                    rhs_scale=w_scales[i],
                     start=(i == 0),
                     stop=False,
                 )
@@ -313,19 +316,16 @@ def tile_gaussiankernel_k_kernel(tc, x, grid, spline_weight, out):
             vector_exponents(i)
         for i in range(W_AHEAD):
             group_w(i)
-            if i > 0:
-                quantise_w(i - 1)
-        banks = turn_quad(0)
+            if i == 2:
+                quantise_w_pair(0)
+        turned = [turn_quad(a) for a in range(2)]
         for i in range(1, MIX_AHEAD):
             mixed_exponents(i)
         for i in range(n_pass - 1):
             g_ = passes[i][0]
-            quad = 0 if i == 0 else i // 8 + 1 if i % 8 == 2 else A_QUADS
-            if 0 < quad < A_QUADS:
-                banks = turn_quad(quad)
             if i + MIX_AHEAD < n_pass:
                 mixed_exponents(i + MIX_AHEAD)
-            if i >= MULTIPLY_BEHIND:
+            if i > MULTIPLY_BEHIND:
                 multiply(i - MULTIPLY_BEHIND)
             if i + VECTOR_AHEAD < n_pass:
                 vector_exponents(i + VECTOR_AHEAD)
@@ -334,16 +334,22 @@ def tile_gaussiankernel_k_kernel(tc, x, grid, spline_weight, out):
             if 2 < i + SCALAR_AHEAD < n_pass:
                 scalar_exponents(i + SCALAR_AHEAD)
             make_basis(i)
-            if quad < A_QUADS:
-                spread_quad(quad, banks)
+            if i < 2:
+                spread_quad(i, turned[i])
+                turned.append(turn_quad(i + 2))
+            if i == 2:
+                for a in (2, 3):
+                    spread_quad(a, turned[a])
             if i % R_POINTS == 0 and g_ + 2 < len(groups):
                 load_w(g_ + 2)
-            if i == 0:
+            if i == 2:
                 acc += [acc_pool.tile([P, OUT], F32, name="acc%d" % bt) for bt in range(B_TILES)]
             if i >= 1:
                 quantise_b(i - 1)
-            if i + W_AHEAD - 1 < n_pass:
-                quantise_w(i + W_AHEAD - 1)
+            if i == MULTIPLY_BEHIND:
+                multiply(0)
+            if i % 2 == 0 and i + W_AHEAD - 2 < n_pass:
+                quantise_w_pair(i + W_AHEAD - 2)
 
         last = n_pass - 1
         multiply(last - 2)
@@ -352,28 +358,23 @@ def tile_gaussiankernel_k_kernel(tc, x, grid, spline_weight, out):
         b_codes[last] = work.tile([P, B], U32, name="b_codes", bufs=5, align_bytes=64)
         b_scales[last] = work.tile([P, B], U8, name="b_scales", bufs=5, align_bytes=64)
 
-        def store_rows(bt):
+        for bt in range(B_TILES):
+            b_cols = slice(bt * P, (bt + 1) * P)
+            make_basis(last, bt, bt + 1)
+            nc.vector.quantize_mx(
+                out=b_codes[last][:, b_cols].bitcast(FP8X4), scales=b_scales[last][:, b_cols],
+                in_=basis[last][:, bt * TILE_COLS : (bt + 1) * TILE_COLS],
+            )
+            nc.tensor.matmul_mx(
+                out=acc[bt][:],
+                lhsT=b_codes[last][:, b_cols].bitcast(FP8X4), lhsT_scale=b_scales[last][:, b_cols],
+                rhs=w_codes[last].bitcast(FP8X4), rhs_scale=w_scales[last],
+                start=False, stop=True,
+            )
+        for bt in range(B_TILES):
             result = store.tile([P, OUT], F32, name="result")
             if bt % 2 == 0:
                 nc.vector.tensor_copy(out=result[:], in_=acc[bt][:])
             else:
                 nc.scalar.copy(out=result[:], in_=acc[bt][:])
             nc.sync.dma_start(out=out[bt * P : (bt + 1) * P, :], in_=result[:])
-
-        for bt in range(B_TILES):
-            b_cols = slice(bt * P, (bt + 1) * P)
-            cols = slice(bt * TILE_COLS, (bt + 1) * TILE_COLS)
-            make_basis(last, bt, bt + 1)
-            nc.vector.quantize_mx(
-                out=b_codes[last][:, b_cols].bitcast(FP8X4), scales=b_scales[last][:, b_cols],
-                in_=basis[last][:, cols],
-            )
-            nc.tensor.matmul_mx(
-                out=acc[bt][:],
-                lhsT=b_codes[last][:, b_cols].bitcast(FP8X4), lhsT_scale=b_scales[last][:, b_cols],
-                rhs=w_codes[last][:].bitcast(FP8X4), rhs_scale=w_scales[last][:],
-                start=False, stop=True,
-            )
-            if bt > 0:
-                store_rows(bt - 1)
-        store_rows(B_TILES - 1)

@@ -27,24 +27,18 @@ TILE_COLS = P * T_PACK
 def tile_gaussiankernel_k_kernel(tc, x, grid, spline_weight, out):
     nc = tc.nc
     groups = [(a, s) for a in range(A_QUADS) for s in range(S_HALVES)]
-    passes = [(g, r) for g in range(len(groups)) for r in (0, 1, 3, 2)]
+    first = [(2, 0, 4), (0, 4, 4), (1, 2, 4), (3, 2, 4)]
+    middle = [(0, 4, 4), (1, 0, 2), (3, 1, 2), (2, 0, 2)]
+    final = [(0, 4, 4), (1, 2, 4), (3, 2, 4), (2, 1, 4)]
+    plans = [first] + [middle] * (len(groups) - 2) + [final]
+    passes = [(g, r, v, m) for g in range(len(groups)) for r, v, m in plans[g]]
     n_pass = len(passes)
-
-    def plan(i):
-        g_, r = passes[i]
-        if r == 0:
-            return B_TILES, B_TILES
-        if g_ == len(groups) - 1:
-            return 2, B_TILES
-        if r == 3:
-            return 2, B_TILES - 1 if g_ < len(groups) // 2 else B_TILES
-        return 0, B_TILES - 2
 
     with ExitStack() as ctx:
         const = ctx.enter_context(tc.tile_pool(name="const", bufs=1))
         xin = ctx.enter_context(tc.tile_pool(name="xin", bufs=B_TILES))
         xgrp = ctx.enter_context(tc.tile_pool(name="xgrp", bufs=1))
-        wload = ctx.enter_context(tc.tile_pool(name="wload", bufs=3))
+        wload = ctx.enter_context(tc.tile_pool(name="wload", bufs=2))
         work = ctx.enter_context(tc.tile_pool(name="work", bufs=4))
         store = ctx.enter_context(tc.tile_pool(name="store", bufs=B_TILES))
         acc_pool = ctx.enter_context(tc.psum_pool(name="acc", bufs=1))
@@ -55,24 +49,25 @@ def tile_gaussiankernel_k_kernel(tc, x, grid, spline_weight, out):
             "(s q a t l r) o -> s a l q t r o",
             s=S_HALVES, q=Q_CHUNKS, a=A_QUADS, t=T_PACK, l=L_HALVES, r=R_POINTS,
         )
-        w_raw = {}
+        w_rows = {}
 
         def load_w(g):
             a, s = groups[g]
-            w_raw[g] = wload.tile([P, T_PACK, R_POINTS, OUT], BF16, name="w_raw")
+            w_raw = wload.tile([P, T_PACK, R_POINTS, OUT], BF16, name="w_raw")
             for l in range(L_HALVES):
                 nc.sync.dma_start(
-                    out=w_raw[g][l:P:L_HALVES].rearrange("q t r o -> q t (r o)"),
+                    out=w_raw[l:P:L_HALVES].rearrange("q t r o -> q t (r o)"),
                     in_=w_view[s, a, l].rearrange("q t r o -> q t (r o)"),
                 )
+            for i in range(g * R_POINTS, (g + 1) * R_POINTS):
+                w_rows[i] = w_raw[:, :, passes[i][1], :]
 
-        def load_w_pass(i):
-            g_, r = passes[i]
-            a, s = groups[g_]
-            if g_ not in w_raw:
-                w_raw[g_] = wload.tile([P, T_PACK, R_POINTS, OUT], BF16, name="w_raw")
+        def load_first_w(i):
+            r = passes[i][1]
+            w_pass = wload.tile([P, T_PACK, OUT], BF16, name="w_pass", bufs=R_POINTS)
             for l in range(L_HALVES):
-                nc.sync.dma_start(out=w_raw[g_][l:P:L_HALVES, :, r, :], in_=w_view[s, a, l, :, :, r, :])
+                nc.sync.dma_start(out=w_pass[l:P:L_HALVES], in_=w_view[0, 0, l, :, :, r, :])
+            w_rows[i] = w_pass[:]
 
         grid_row = const.tile([P, G], BF16)
         nc.vector.memset(grid_row[:], 0.0)
@@ -87,7 +82,7 @@ def tile_gaussiankernel_k_kernel(tc, x, grid, spline_weight, out):
                     in_=x[bt * P : (bt + 1) * P, s * (IN // S_HALVES) : (s + 1) * (IN // S_HALVES)],
                 )
             for i in range(2 * s, 2 * s + 2):
-                load_w_pass(i)
+                load_first_w(i)
         load_w(1)
 
         ident = const.tile([P, P], F32)
@@ -137,7 +132,7 @@ def tile_gaussiankernel_k_kernel(tc, x, grid, spline_weight, out):
             ]
 
         def spread_quad(a, banks):
-            x_turned = work.tile([P, COLS], BF16, name="x_turned")
+            x_turned = work.tile([P, COLS], BF16, name="x_turned", bufs=3)
             for h in range(2):
                 copy_half(x_turned, banks[h], h)
             for g_ in range(len(groups)):
@@ -153,12 +148,11 @@ def tile_gaussiankernel_k_kernel(tc, x, grid, spline_weight, out):
         exponent_0, on_vector, on_scalar, mixed = {}, {}, {}, {}
 
         def group_w(i):
-            g_, r = passes[i]
             if i % 2 == 0:
                 w_grouped[i] = work.tile([P, 2, OUT, T_PACK], BF16, name="w_grouped", bufs=2, align_bytes=64)
             nc.vector.tensor_copy(
                 out=w_grouped[i - i % 2][:, i % 2].rearrange("p (c i) t -> p c t i", i=4),
-                in_=w_raw[g_][:, :, r, :].rearrange("p t (c i) -> p c t i", i=4),
+                in_=w_rows[i].rearrange("p t (c i) -> p c t i", i=4),
             )
 
         def quantise_w_pair(i):
@@ -173,8 +167,7 @@ def tile_gaussiankernel_k_kernel(tc, x, grid, spline_weight, out):
                 w_codes[i + j], w_scales[i + j] = codes[:, j], scales[:, j]
 
         def vector_exponents(i):
-            g_, r = passes[i]
-            v, m = plan(i)
+            g_, r, v, m = passes[i]
             if v == 0:
                 return
             if r == 0:
@@ -189,19 +182,22 @@ def tile_gaussiankernel_k_kernel(tc, x, grid, spline_weight, out):
             )
 
         def scalar_exponents(i):
-            g_, r = passes[i]
-            v, m = plan(i)
+            g_, r, v, m = passes[i]
             if m == v:
                 return
-            on_scalar[i] = work.tile([P, COLS // 2], F32, name="on_scalar", bufs=3)
+            on_scalar[i] = work.tile([P, 3 * TILE_COLS], F32, name="on_scalar", bufs=2)
+            square(i, v, m)
+
+        def square(i, t0, t1):
+            g_, r, v, m = passes[i]
             nc.scalar.activation(
-                out=on_scalar[i][:, : (m - v) * TILE_COLS], in_=xq[g_][:, v * TILE_COLS : m * TILE_COLS],
+                out=on_scalar[i][:, (t0 - v) * TILE_COLS : (t1 - v) * TILE_COLS],
+                in_=xq[g_][:, t0 * TILE_COLS : t1 * TILE_COLS],
                 func=ACT.Square, bias=neg_g[:, r : r + 1], scale=1.0,
             )
 
         def mixed_exponents(i):
-            g_, r = passes[i]
-            v, m = plan(i)
+            g_, r, v, m = passes[i]
             mixed[i] = {}
             for bt in range(m, B_TILES):
                 bank = bank_pool.tile([P, TILE_COLS], F32, name="bank")
@@ -212,8 +208,7 @@ def tile_gaussiankernel_k_kernel(tc, x, grid, spline_weight, out):
                 mixed[i][bt] = bank
 
         def make_basis(i, first=0, end=B_TILES):
-            g_, r = passes[i]
-            v, m = plan(i)
+            g_, r, v, m = passes[i]
             if first == 0:
                 basis[i] = work.tile([P, COLS], BF16, name="basis", align_bytes=64)
 
@@ -279,9 +274,19 @@ def tile_gaussiankernel_k_kernel(tc, x, grid, spline_weight, out):
             out=neg_g2_h2[:], in0=g[:], scalar=-INV_H2, in1=g[:], op0=ALU.mult, op1=ALU.mult
         )
 
+        on_scalar[0] = work.tile([P, COLS], F32, name="exponent_0", bufs=2)
         for h in range(2):
             bank = turn_half(lambda bt, u: x_twice[bt][:, u].rearrange("b q l -> b (q l)"), h)
             copy_half(xq[0], bank, h)
+            square(0, 2 * h, 2 * h + 2)
+        turned = [turn_quad(a) for a in range(2)]
+        group_w(0)
+        vector_exponents(1)
+        group_w(1)
+        quantise_w_pair(0)
+        vector_exponents(2)
+        group_w(2)
+
         share = const.tile([P, G], F32)
         nc.vector.tensor_scalar(
             out=share[:], in0=g_all[:], scalar1=g_all[:, 0:1], scalar2=None, op0=ALU.subtract
@@ -298,29 +303,17 @@ def tile_gaussiankernel_k_kernel(tc, x, grid, spline_weight, out):
             mix[r] = const.tile([P, P], F32, name="mix%d" % r)
             for l in range(L_HALVES):
                 j = R_POINTS * l + r
-                nc.vector.tensor_scalar_mul(
+                nc.gpsimd.tensor_scalar(
                     out=mix[r][:].rearrange("p (q l) -> p q l", l=L_HALVES)[:, :, l],
-                    in0=same_q[:], scalar1=weight[:, j : j + 1],
+                    in0=same_q[:], scalar1=weight[:, j : j + 1], scalar2=None, op0=ALU.mult,
                 )
-
-        vector_exponents(0)
-        scalar_exponents(1)
-        scalar_exponents(2)
+        group_w(3)
 
         W_AHEAD = 4
         VECTOR_AHEAD = 3
-        SCALAR_AHEAD = 2
+        SCALAR_AHEAD = 1
         MIX_AHEAD = 2
         MULTIPLY_BEHIND = 2
-        for i in range(1, VECTOR_AHEAD):
-            vector_exponents(i)
-        for i in range(W_AHEAD):
-            group_w(i)
-            if i == 2:
-                quantise_w_pair(0)
-        turned = [turn_quad(a) for a in range(2)]
-        for i in range(1, MIX_AHEAD):
-            mixed_exponents(i)
         for i in range(n_pass - 1):
             g_ = passes[i][0]
             if i + MIX_AHEAD < n_pass:
@@ -331,7 +324,7 @@ def tile_gaussiankernel_k_kernel(tc, x, grid, spline_weight, out):
                 vector_exponents(i + VECTOR_AHEAD)
             if i + W_AHEAD < n_pass:
                 group_w(i + W_AHEAD)
-            if 2 < i + SCALAR_AHEAD < n_pass:
+            if i + SCALAR_AHEAD < n_pass:
                 scalar_exponents(i + SCALAR_AHEAD)
             make_basis(i)
             if i < 2:
@@ -340,7 +333,7 @@ def tile_gaussiankernel_k_kernel(tc, x, grid, spline_weight, out):
             if i == 2:
                 for a in (2, 3):
                     spread_quad(a, turned[a])
-            if i % R_POINTS == 0 and g_ + 2 < len(groups):
+            if i == 1 or i % R_POINTS == 0 and 0 < g_ < len(groups) - 2:
                 load_w(g_ + 2)
             if i == 2:
                 acc += [acc_pool.tile([P, OUT], F32, name="acc%d" % bt) for bt in range(B_TILES)]

@@ -27,9 +27,9 @@ TILE_COLS = P * T_PACK
 def tile_gaussiankernel_k_kernel(tc, x, grid, spline_weight, out):
     nc = tc.nc
     groups = [(a, s) for a in range(A_QUADS) for s in range(S_HALVES)]
-    first = [(2, 0, 4), (0, 4, 4), (1, 2, 4), (3, 2, 4)]
-    middle = [(0, 4, 4), (1, 0, 2), (3, 1, 2), (2, 0, 2)]
-    final = [(0, 4, 4), (1, 2, 4), (3, 2, 4), (2, 1, 4)]
+    first = [(2, 0, 4), (0, 4, 4), (1, 2, 4), (3, 2, 3)]
+    middle = [(0, 4, 4), (1, 0, 2), (3, 2, 4), (2, 0, 2)]
+    final = [(0, 4, 4), (1, 1, 3), (3, 2, 4), (2, 2, 4)]
     plans = [first] + [middle] * (len(groups) - 2) + [final]
     passes = [(g, r, v, m) for g in range(len(groups)) for r, v, m in plans[g]]
     n_pass = len(passes)
@@ -38,7 +38,7 @@ def tile_gaussiankernel_k_kernel(tc, x, grid, spline_weight, out):
         const = ctx.enter_context(tc.tile_pool(name="const", bufs=1))
         xin = ctx.enter_context(tc.tile_pool(name="xin", bufs=B_TILES))
         xgrp = ctx.enter_context(tc.tile_pool(name="xgrp", bufs=1))
-        wload = ctx.enter_context(tc.tile_pool(name="wload", bufs=2))
+        wload = ctx.enter_context(tc.tile_pool(name="wload", bufs=3))
         work = ctx.enter_context(tc.tile_pool(name="work", bufs=4))
         store = ctx.enter_context(tc.tile_pool(name="store", bufs=B_TILES))
         acc_pool = ctx.enter_context(tc.psum_pool(name="acc", bufs=1))
@@ -132,7 +132,7 @@ def tile_gaussiankernel_k_kernel(tc, x, grid, spline_weight, out):
             ]
 
         def spread_quad(a, banks):
-            x_turned = work.tile([P, COLS], BF16, name="x_turned", bufs=3)
+            x_turned = work.tile([P, COLS], BF16, name="x_turned", bufs=2)
             for h in range(2):
                 copy_half(x_turned, banks[h], h)
             for g_ in range(len(groups)):
@@ -174,7 +174,7 @@ def tile_gaussiankernel_k_kernel(tc, x, grid, spline_weight, out):
                 exponent_0[g_] = work.tile([P, COLS], F32, name="exponent_0", bufs=2)
                 on_vector[i] = exponent_0[g_]
             else:
-                on_vector[i] = work.tile([P, COLS // 2], F32, name="on_vector", bufs=3)
+                on_vector[i] = work.tile([P, COLS // 2], F32, name="on_vector", bufs=2)
             cols = slice(0, v * TILE_COLS)
             nc.vector.scalar_tensor_tensor(
                 out=on_vector[i][:, cols], in0=xq[g_][:, cols], scalar=two_g[:, r : r + 1], in1=xq[g_][:, cols],
@@ -303,9 +303,9 @@ def tile_gaussiankernel_k_kernel(tc, x, grid, spline_weight, out):
             mix[r] = const.tile([P, P], F32, name="mix%d" % r)
             for l in range(L_HALVES):
                 j = R_POINTS * l + r
-                nc.gpsimd.tensor_scalar(
+                nc.vector.tensor_scalar_mul(
                     out=mix[r][:].rearrange("p (q l) -> p q l", l=L_HALVES)[:, :, l],
-                    in0=same_q[:], scalar1=weight[:, j : j + 1], scalar2=None, op0=ALU.mult,
+                    in0=same_q[:], scalar1=weight[:, j : j + 1],
                 )
         group_w(3)
 

@@ -28,8 +28,8 @@ def tile_gaussiankernel_k_kernel(tc, x, grid, spline_weight, out):
     nc = tc.nc
     groups = [(a, s) for a in range(A_QUADS) for s in range(S_HALVES)]
     first = [(2, 0, 4), (0, 4, 4), (1, 2, 4), (3, 2, 3)]
-    middle = [(0, 4, 4), (1, 0, 2), (3, 2, 4), (2, 0, 2)]
-    final = [(0, 4, 4), (1, 1, 3), (3, 2, 4), (2, 2, 4)]
+    middle = [(0, 4, 4), (1, 2, 2), (3, 0, 4), (2, 0, 2)]
+    final = [(0, 4, 4), (1, 2, 4), (3, 2, 4), (2, 2, 4)]
     plans = [first] + [middle] * (len(groups) - 2) + [final]
     passes = [(g, r, v, m) for g in range(len(groups)) for r, v, m in plans[g]]
     n_pass = len(passes)
@@ -40,7 +40,6 @@ def tile_gaussiankernel_k_kernel(tc, x, grid, spline_weight, out):
         xgrp = ctx.enter_context(tc.tile_pool(name="xgrp", bufs=1))
         wload = ctx.enter_context(tc.tile_pool(name="wload", bufs=3))
         work = ctx.enter_context(tc.tile_pool(name="work", bufs=4))
-        store = ctx.enter_context(tc.tile_pool(name="store", bufs=B_TILES))
         acc_pool = ctx.enter_context(tc.psum_pool(name="acc", bufs=1))
         bank_pool = ctx.enter_context(tc.psum_pool(name="banks", bufs=4))
         ctx.enter_context(tc.manual_schedule())
@@ -174,7 +173,7 @@ def tile_gaussiankernel_k_kernel(tc, x, grid, spline_weight, out):
                 exponent_0[g_] = work.tile([P, COLS], F32, name="exponent_0", bufs=2)
                 on_vector[i] = exponent_0[g_]
             else:
-                on_vector[i] = work.tile([P, COLS // 2], F32, name="on_vector", bufs=2)
+                on_vector[i] = work.tile([P, COLS // 2], F32, name="on_vector", bufs=3)
             cols = slice(0, v * TILE_COLS)
             nc.vector.scalar_tensor_tensor(
                 out=on_vector[i][:, cols], in0=xq[g_][:, cols], scalar=two_g[:, r : r + 1], in1=xq[g_][:, cols],
@@ -185,7 +184,7 @@ def tile_gaussiankernel_k_kernel(tc, x, grid, spline_weight, out):
             g_, r, v, m = passes[i]
             if m == v:
                 return
-            on_scalar[i] = work.tile([P, 3 * TILE_COLS], F32, name="on_scalar", bufs=2)
+            on_scalar[i] = work.tile([P, COLS], F32, name="on_scalar", bufs=2)
             square(i, v, m)
 
         def square(i, t0, t1):
@@ -274,7 +273,7 @@ def tile_gaussiankernel_k_kernel(tc, x, grid, spline_weight, out):
             out=neg_g2_h2[:], in0=g[:], scalar=-INV_H2, in1=g[:], op0=ALU.mult, op1=ALU.mult
         )
 
-        on_scalar[0] = work.tile([P, COLS], F32, name="exponent_0", bufs=2)
+        on_scalar[0] = work.tile([P, COLS], F32, name="on_scalar", bufs=2)
         for h in range(2):
             bank = turn_half(lambda bt, u: x_twice[bt][:, u].rearrange("b q l -> b (q l)"), h)
             copy_half(xq[0], bank, h)
@@ -365,7 +364,7 @@ def tile_gaussiankernel_k_kernel(tc, x, grid, spline_weight, out):
                 start=False, stop=True,
             )
         for bt in range(B_TILES):
-            result = store.tile([P, OUT], F32, name="result")
+            result = work.tile([P, OUT], F32, name="basis", align_bytes=64)
             if bt % 2 == 0:
                 nc.vector.tensor_copy(out=result[:], in_=acc[bt][:])
             else:

@@ -27,10 +27,11 @@ TILE_COLS = P * T_PACK
 def tile_gaussiankernel_k_kernel(tc, x, grid, spline_weight, out):
     nc = tc.nc
     groups = [(a, s) for a in range(A_QUADS) for s in range(S_HALVES)]
-    first = [(2, 0, 4), (0, 4, 4), (1, 2, 4), (3, 2, 3)]
-    middle = [(0, 4, 4), (1, 2, 2), (3, 0, 4), (2, 0, 2)]
-    final = [(0, 4, 4), (1, 2, 4), (3, 2, 4), (2, 2, 4)]
-    plans = [first] + [middle] * (len(groups) - 2) + [final]
+    first = [(2, 0, 4), (0, 4, 4), (1, 2, 4), (3, 1, 2)]
+    odd_middle = [(0, 4, 4), (1, 1, 2), (3, 0, 3), (2, 0, 2)]
+    even_middle = [(0, 4, 4), (1, 2, 2), (3, 0, 4), (2, 0, 2)]
+    final = [(0, 4, 4), (1, 1, 3), (3, 1, 4), (2, 2, 4)]
+    plans = [first] + [odd_middle, even_middle] * ((len(groups) - 2) // 2) + [final]
     passes = [(g, r, v, m) for g in range(len(groups)) for r, v, m in plans[g]]
     n_pass = len(passes)
 
@@ -235,8 +236,8 @@ def tile_gaussiankernel_k_kernel(tc, x, grid, spline_weight, out):
 
         acc = []
 
-        def multiply(i):
-            for bt in range(B_TILES):
+        def multiply(i, row_tiles=range(B_TILES)):
+            for bt in row_tiles:
                 b_cols = slice(bt * P, (bt + 1) * P)
                 nc.tensor.matmul_mx(
                     out=acc[bt][:],
@@ -245,7 +246,7 @@ def tile_gaussiankernel_k_kernel(tc, x, grid, spline_weight, out):
                     rhs=w_codes[i].bitcast(FP8X4),
                     rhs_scale=w_scales[i],
                     start=(i == 0),
-                    stop=False,
+                    stop=(i == n_pass - 1),
                 )
 
         x_twice = []
@@ -346,7 +347,6 @@ def tile_gaussiankernel_k_kernel(tc, x, grid, spline_weight, out):
         last = n_pass - 1
         multiply(last - 2)
         quantise_b(last - 1)
-        multiply(last - 1)
         b_codes[last] = work.tile([P, B], U32, name="b_codes", bufs=5, align_bytes=64)
         b_scales[last] = work.tile([P, B], U8, name="b_scales", bufs=5, align_bytes=64)
 
@@ -357,12 +357,8 @@ def tile_gaussiankernel_k_kernel(tc, x, grid, spline_weight, out):
                 out=b_codes[last][:, b_cols].bitcast(FP8X4), scales=b_scales[last][:, b_cols],
                 in_=basis[last][:, bt * TILE_COLS : (bt + 1) * TILE_COLS],
             )
-            nc.tensor.matmul_mx(
-                out=acc[bt][:],
-                lhsT=b_codes[last][:, b_cols].bitcast(FP8X4), lhsT_scale=b_scales[last][:, b_cols],
-                rhs=w_codes[last].bitcast(FP8X4), rhs_scale=w_scales[last],
-                start=False, stop=True,
-            )
+            multiply(last - 1, [bt])
+            multiply(last, [bt])
         for bt in range(B_TILES):
             result = work.tile([P, OUT], F32, name="basis", align_bytes=64)
             if bt % 2 == 0:

from contextlib import ExitStack

import concourse.mybir as mybir
from concourse.masks import make_identity

F32 = mybir.dt.float32
BF16 = mybir.dt.bfloat16
U32 = mybir.dt.uint32
U8 = mybir.dt.uint8
FP8X4 = mybir.dt.float8_e4m3fn_x4
ACT = mybir.ActivationFunctionType
ALU = mybir.AluOpType
AX = mybir.AxisListType

P = 128
B, IN, G, OUT = 512, 2048, 8, 512
K = IN * G
FLOPS = 2 * B * K * OUT
INV_H2 = 49.0 / 16.0

S_HALVES, Q_CHUNKS, A_QUADS, T_PACK, L_HALVES, R_POINTS = 2, 64, 4, 4, 2, 4
B_TILES = B // P
COLS = B * T_PACK
TILE_COLS = P * T_PACK


def tile_gaussiankernel_k_kernel(tc, x, grid, spline_weight, out):
    nc = tc.nc
    groups = [(a, s) for a in range(A_QUADS) for s in range(S_HALVES)]
    first = [(2, 0, 4), (0, 4, 4), (1, 2, 4), (3, 1, 2)]
    odd_middle = [(0, 4, 4), (1, 1, 2), (3, 0, 3), (2, 0, 2)]
    even_middle = [(0, 4, 4), (1, 2, 2), (3, 0, 4), (2, 0, 2)]
    final = [(0, 4, 4), (1, 1, 3), (3, 1, 4), (2, 2, 4)]
    plans = [first] + [odd_middle, even_middle] * ((len(groups) - 2) // 2) + [final]
    passes = [(g, r, v, m) for g in range(len(groups)) for r, v, m in plans[g]]
    n_pass = len(passes)

    with ExitStack() as ctx:
        const = ctx.enter_context(tc.tile_pool(name="const", bufs=1))
        xin = ctx.enter_context(tc.tile_pool(name="xin", bufs=B_TILES))
        xgrp = ctx.enter_context(tc.tile_pool(name="xgrp", bufs=1))
        wload = ctx.enter_context(tc.tile_pool(name="wload", bufs=3))
        work = ctx.enter_context(tc.tile_pool(name="work", bufs=4))
        acc_pool = ctx.enter_context(tc.psum_pool(name="acc", bufs=1))
        bank_pool = ctx.enter_context(tc.psum_pool(name="banks", bufs=4))
        ctx.enter_context(tc.manual_schedule())

        w_view = spline_weight.rearrange(
            "(s q a t l r) o -> s a l q t r o",
            s=S_HALVES, q=Q_CHUNKS, a=A_QUADS, t=T_PACK, l=L_HALVES, r=R_POINTS,
        )
        w_rows = {}

        def load_w(g):
            a, s = groups[g]
            w_raw = wload.tile([P, T_PACK, R_POINTS, OUT], BF16, name="w_raw")
            for l in range(L_HALVES):
                nc.sync.dma_start(
                    out=w_raw[l:P:L_HALVES].rearrange("q t r o -> q t (r o)"),
                    in_=w_view[s, a, l].rearrange("q t r o -> q t (r o)"),
                )
            for i in range(g * R_POINTS, (g + 1) * R_POINTS):
                w_rows[i] = w_raw[:, :, passes[i][1], :]

        def load_first_w(i):
            r = passes[i][1]
            w_pass = wload.tile([P, T_PACK, OUT], BF16, name="w_pass", bufs=R_POINTS)
            for l in range(L_HALVES):
                nc.sync.dma_start(out=w_pass[l:P:L_HALVES], in_=w_view[0, 0, l, :, :, r, :])
            w_rows[i] = w_pass[:]

        grid_row = const.tile([P, G], BF16)
        nc.vector.memset(grid_row[:], 0.0)
        nc.sync.dma_start(out=grid_row[0:1, :], in_=grid.unsqueeze(0))
        ones = const.tile([P, P], BF16)
        nc.gpsimd.memset(ones[:], 1.0)
        x_rows = [xin.tile([P, S_HALVES, IN // S_HALVES], BF16, name="x_rows") for bt in range(B_TILES)]
        for s in range(S_HALVES):
            for bt in range(B_TILES):
                nc.sync.dma_start(
                    out=x_rows[bt][:, s, :],
                    in_=x[bt * P : (bt + 1) * P, s * (IN // S_HALVES) : (s + 1) * (IN // S_HALVES)],
                )
            for i in range(2 * s, 2 * s + 2):
                load_first_w(i)
        load_w(1)

        ident = const.tile([P, P], F32)
        make_identity(nc, ident[:])
        ident_ql = ident[:].rearrange("p (q l) -> p q l", l=L_HALVES)
        odd = const.tile([P, 1], F32)
        nc.vector.reduce_sum(out=odd[:], in_=ident_ql[:, :, 1], axis=AX.X)
        even = const.tile([P, 1], F32)
        nc.vector.tensor_scalar(out=even[:], in0=odd[:], scalar1=-1.0, scalar2=1.0, op0=ALU.mult, op1=ALU.add)
        sign = const.tile([P, 1], F32)
        nc.vector.tensor_sub(out=sign[:], in0=odd[:], in1=even[:])
        same_q = const.tile([P, Q_CHUNKS], F32)
        nc.vector.tensor_add(out=same_q[:], in0=ident_ql[:, :, 0], in1=ident_ql[:, :, 1])

        grid_bank = acc_pool.tile([P, G], F32, name="acc3")
        nc.tensor.matmul(grid_bank[:], lhsT=ones[:], rhs=grid_row[:], start=True, stop=True)

        def words(bt, s):
            return x_rows[bt][:, s, :].bitcast(F32).rearrange("b (q c) -> b c q", c=8)

        def turn_half(words_of, h, bank=None):
            if bank is None:
                bank = bank_pool.tile([P, 2, 2 * P], F32, name="bank")
            for u in range(2):
                for e in range(2):
                    nc.tensor.transpose(bank[:, u, e * P : (e + 1) * P], words_of(2 * h + e, u), ident[:])
            return bank

        def copy_half(dst, bank, h):
            nc.scalar.copy(
                out=dst[:].bitcast(F32).rearrange("p (b u) -> p b u", u=2)[:, 2 * P * h : 2 * P * (h + 1), :],
                in_=bank[:].rearrange("p u b -> p b u"),
            )

        xq = [xgrp.tile([P, COLS], BF16, name="xq%d" % i) for i in range(len(groups))]

        def turn_quad(a):
            def words_of(bt, u):
                return (
                    x_rows[bt][:].rearrange("b s i -> b (s i)").bitcast(F32)
                    .rearrange("b (Q c) -> b c Q", c=8)[:, 2 * a + u, :]
                )

            return [
                turn_half(words_of, h, acc_pool.tile([P, 2, 2 * P], F32, name="acc%d" % (2 * (a % 2) + h)))
                for h in range(2)
            ]

        def spread_quad(a, banks):
            x_turned = work.tile([P, COLS], BF16, name="x_turned", bufs=2)
            for h in range(2):
                copy_half(x_turned, banks[h], h)
            for g_ in range(len(groups)):
                if groups[g_][0] == a and g_ > 0:
                    s = groups[g_][1]
                    for l in range(L_HALVES):
                        nc.sync.dma_start(
                            out=xq[g_][l:P:L_HALVES, :],
                            in_=x_turned[Q_CHUNKS * s : Q_CHUNKS * (s + 1), :],
                        )

        w_grouped, w_codes, w_scales, basis, b_codes, b_scales = {}, {}, {}, {}, {}, {}
        exponent_0, on_vector, on_scalar, mixed = {}, {}, {}, {}

        def group_w(i):
            if i % 2 == 0:
                w_grouped[i] = work.tile([P, 2, OUT, T_PACK], BF16, name="w_grouped", bufs=2, align_bytes=64)
            nc.vector.tensor_copy(
                out=w_grouped[i - i % 2][:, i % 2].rearrange("p (c i) t -> p c t i", i=4),
                in_=w_rows[i].rearrange("p t (c i) -> p c t i", i=4),
            )

        def quantise_w_pair(i):
            codes = work.tile([P, 2, OUT], U32, name="w_codes", align_bytes=64)
            scales = work.tile([P, 2, OUT], U8, name="w_scales", align_bytes=64)
            nc.vector.quantize_mx(
                out=codes[:].rearrange("p j o -> p (j o)").bitcast(FP8X4),
                scales=scales[:].rearrange("p j o -> p (j o)"),
                in_=w_grouped[i][:].rearrange("p j o t -> p (j o t)"),
            )
            for j in range(2):
                w_codes[i + j], w_scales[i + j] = codes[:, j], scales[:, j]

        def vector_exponents(i):
            g_, r, v, m = passes[i]
            if v == 0:
                return
            if r == 0:
                exponent_0[g_] = work.tile([P, COLS], F32, name="exponent_0", bufs=2)
                on_vector[i] = exponent_0[g_]
            else:
                on_vector[i] = work.tile([P, COLS // 2], F32, name="on_vector", bufs=3)
            cols = slice(0, v * TILE_COLS)
            nc.vector.scalar_tensor_tensor(
                out=on_vector[i][:, cols], in0=xq[g_][:, cols], scalar=two_g[:, r : r + 1], in1=xq[g_][:, cols],
                op0=ALU.subtract, op1=ALU.mult,
            )

        def scalar_exponents(i):
            g_, r, v, m = passes[i]
            if m == v:
                return
            on_scalar[i] = work.tile([P, COLS], F32, name="on_scalar", bufs=2)
            square(i, v, m)

        def square(i, t0, t1):
            g_, r, v, m = passes[i]
            nc.scalar.activation(
                out=on_scalar[i][:, (t0 - v) * TILE_COLS : (t1 - v) * TILE_COLS],
                in_=xq[g_][:, t0 * TILE_COLS : t1 * TILE_COLS],
                func=ACT.Square, bias=neg_g[:, r : r + 1], scale=1.0,
            )

        def mixed_exponents(i):
            g_, r, v, m = passes[i]
            mixed[i] = {}
            for bt in range(m, B_TILES):
                bank = bank_pool.tile([P, TILE_COLS], F32, name="bank")
                nc.tensor.matmul(
                    bank[:], lhsT=mix[r][:], rhs=exponent_0[g_][:, bt * TILE_COLS : (bt + 1) * TILE_COLS],
                    start=True, stop=True,
                )
                mixed[i][bt] = bank

        def make_basis(i, first=0, end=B_TILES):
            g_, r, v, m = passes[i]
            if first == 0:
                basis[i] = work.tile([P, COLS], BF16, name="basis", align_bytes=64)

            def exp(t0, t1, source, bias):
                nc.scalar.activation(
                    out=basis[i][:, t0 * TILE_COLS : t1 * TILE_COLS], in_=source,
                    func=ACT.Exp, bias=bias, scale=-INV_H2,
                )

            t0, t1 = first, min(v, end)
            if t0 < t1:
                exp(t0, t1, on_vector[i][:, t0 * TILE_COLS : t1 * TILE_COLS], neg_g2_h2[:, r : r + 1])
            t0, t1 = max(v, first), min(m, end)
            if t0 < t1:
                exp(t0, t1, on_scalar[i][:, (t0 - v) * TILE_COLS : (t1 - v) * TILE_COLS], 0.0)
            for bt in range(max(m, first), end):
                exp(bt, bt + 1, mixed[i][bt][:], neg_g2_h2[:, r : r + 1])

        def quantise_b(i):
            b_codes[i] = work.tile([P, B], U32, name="b_codes", bufs=5, align_bytes=64)
            b_scales[i] = work.tile([P, B], U8, name="b_scales", bufs=5, align_bytes=64)
            nc.vector.quantize_mx(
                out=b_codes[i][:].bitcast(FP8X4), scales=b_scales[i][:], in_=basis[i][:]
            )

        acc = []

        def multiply(i, row_tiles=range(B_TILES)):
            for bt in row_tiles:
                b_cols = slice(bt * P, (bt + 1) * P)
                nc.tensor.matmul_mx(
                    out=acc[bt][:],
                    lhsT=b_codes[i][:, b_cols].bitcast(FP8X4),
                    lhsT_scale=b_scales[i][:, b_cols],
                    rhs=w_codes[i].bitcast(FP8X4),
                    rhs_scale=w_scales[i],
                    start=(i == 0),
                    stop=(i == n_pass - 1),
                )

        x_twice = []
        for bt in range(B_TILES):
            twice = xin.tile([P, 2, Q_CHUNKS, L_HALVES], F32, name="twice")
            nc.vector.tensor_copy(
                out=twice[:],
                in_=words(bt, 0)[:, 0:2, :].unsqueeze(3).to_broadcast([P, 2, Q_CHUNKS, L_HALVES]),
            )
            x_twice.append(twice)
        g_all = const.tile([P, G], F32)
        nc.vector.tensor_copy(out=g_all[:], in_=grid_bank[:])
        g_odd = const.tile([P, R_POINTS], F32)
        nc.vector.tensor_scalar_mul(out=g_odd[:], in0=g_all[:, R_POINTS:], scalar1=odd[:])
        g = const.tile([P, R_POINTS], F32)
        nc.vector.scalar_tensor_tensor(
            out=g[:], in0=g_all[:, :R_POINTS], scalar=even[:], in1=g_odd[:], op0=ALU.mult, op1=ALU.add
        )
        neg_g = const.tile([P, R_POINTS], F32)
        nc.vector.tensor_scalar_mul(out=neg_g[:], in0=g[:], scalar1=-1.0)
        two_g = const.tile([P, R_POINTS], F32)
        nc.vector.tensor_scalar_mul(out=two_g[:], in0=g[:], scalar1=2.0)
        neg_g2_h2 = const.tile([P, R_POINTS], F32)
        nc.vector.scalar_tensor_tensor(
            out=neg_g2_h2[:], in0=g[:], scalar=-INV_H2, in1=g[:], op0=ALU.mult, op1=ALU.mult
        )

        on_scalar[0] = work.tile([P, COLS], F32, name="on_scalar", bufs=2)
        for h in range(2):
            bank = turn_half(lambda bt, u: x_twice[bt][:, u].rearrange("b q l -> b (q l)"), h)
            copy_half(xq[0], bank, h)
            square(0, 2 * h, 2 * h + 2)
        turned = [turn_quad(a) for a in range(2)]
        group_w(0)
        vector_exponents(1)
        group_w(1)
        quantise_w_pair(0)
        vector_exponents(2)
        group_w(2)

        share = const.tile([P, G], F32)
        nc.vector.tensor_scalar(
            out=share[:], in0=g_all[:], scalar1=g_all[:, 0:1], scalar2=None, op0=ALU.subtract
        )
        inv_span = const.tile([P, 1], F32)
        nc.vector.reciprocal(out=inv_span[:], in_=share[:, R_POINTS : R_POINTS + 1])
        nc.vector.tensor_scalar_mul(out=share[:], in0=share[:], scalar1=inv_span[:])
        weight = const.tile([P, G], F32)
        nc.vector.tensor_scalar(
            out=weight[:], in0=share[:], scalar1=sign[:], scalar2=even[:], op0=ALU.mult, op1=ALU.add
        )
        mix = {}
        for r in range(1, R_POINTS):
            mix[r] = const.tile([P, P], F32, name="mix%d" % r)
            for l in range(L_HALVES):
                j = R_POINTS * l + r
                nc.vector.tensor_scalar_mul(
                    out=mix[r][:].rearrange("p (q l) -> p q l", l=L_HALVES)[:, :, l],
                    in0=same_q[:], scalar1=weight[:, j : j + 1],
                )
        group_w(3)

        W_AHEAD = 4
        VECTOR_AHEAD = 3
        SCALAR_AHEAD = 1
        MIX_AHEAD = 2
        MULTIPLY_BEHIND = 2
        for i in range(n_pass - 1):
            g_ = passes[i][0]
            if i + MIX_AHEAD < n_pass:
                mixed_exponents(i + MIX_AHEAD)
            if i > MULTIPLY_BEHIND:
                multiply(i - MULTIPLY_BEHIND)
            if i + VECTOR_AHEAD < n_pass:
                vector_exponents(i + VECTOR_AHEAD)
            if i + W_AHEAD < n_pass:
                group_w(i + W_AHEAD)
            if i + SCALAR_AHEAD < n_pass:
                scalar_exponents(i + SCALAR_AHEAD)
            make_basis(i)
            if i < 2:
                spread_quad(i, turned[i])
                turned.append(turn_quad(i + 2))
            if i == 2:
                for a in (2, 3):
                    spread_quad(a, turned[a])
            if i == 1 or i % R_POINTS == 0 and 0 < g_ < len(groups) - 2:
                load_w(g_ + 2)
            if i == 2:
                acc += [acc_pool.tile([P, OUT], F32, name="acc%d" % bt) for bt in range(B_TILES)]
            if i >= 1:
                quantise_b(i - 1)
            if i == MULTIPLY_BEHIND:
                multiply(0)
            if i % 2 == 0 and i + W_AHEAD - 2 < n_pass:
                quantise_w_pair(i + W_AHEAD - 2)

        last = n_pass - 1
        multiply(last - 2)
        quantise_b(last - 1)
        b_codes[last] = work.tile([P, B], U32, name="b_codes", bufs=5, align_bytes=64)
        b_scales[last] = work.tile([P, B], U8, name="b_scales", bufs=5, align_bytes=64)

        for bt in range(B_TILES):
            b_cols = slice(bt * P, (bt + 1) * P)
            make_basis(last, bt, bt + 1)
            nc.vector.quantize_mx(
                out=b_codes[last][:, b_cols].bitcast(FP8X4), scales=b_scales[last][:, b_cols],
                in_=basis[last][:, bt * TILE_COLS : (bt + 1) * TILE_COLS],
            )
            multiply(last - 1, [bt])
            multiply(last, [bt])
        for bt in range(B_TILES):
            result = work.tile([P, OUT], F32, name="basis", align_bytes=64)
            if bt % 2 == 0:
                nc.vector.tensor_copy(out=result[:], in_=acc[bt][:])
            else:
                nc.scalar.copy(out=result[:], in_=acc[bt][:])
            nc.sync.dma_start(out=out[bt * P : (bt + 1) * P, :], in_=result[:])
